import numpy as np
import ml_dtypes


def mxq(x, axis, fmt="e4m3"):
    dtype, down = {"e4m3": (ml_dtypes.float8_e4m3fn, 7), "e5m2": (ml_dtypes.float8_e5m2, 14)}[fmt]
    v = np.moveaxis(np.asarray(x, np.float32).astype(ml_dtypes.bfloat16).astype(np.float64), axis, -1)
    blocks = v.reshape(v.shape[:-1] + (-1, 32))
    amax = np.abs(blocks).max(-1, keepdims=True)
    byte = np.maximum(np.where(amax > 0, np.frexp(amax)[1] - 1 + 127, 0) - down, 1)
    scale = np.exp2(byte - 127.0)
    codes = (blocks / scale).astype(np.float32).astype(dtype).astype(np.float64)
    return np.moveaxis((codes * scale).reshape(v.shape), -1, axis)


WIDE = False


def mx_kscale(k):
    if not WIDE:
        return np.ones(k)
    levels = np.array([10, -10, 5, -5, 0])
    a = np.random.permutation(np.resize(levels, k // 512 * 4)).reshape(k // 512, 4)
    idx = np.arange(k)
    return np.exp2(a[idx // 512, idx % 128 // 32])


BF16 = ml_dtypes.bfloat16


def bf(x):
    return np.asarray(x, np.float32).astype(BF16)


def f64(x):
    return np.asarray(x).astype(np.float64)


B, I, J, C = 8192, 32, 256, 32
K = C * I
HSTEP = 2.0 / (C - 1)
PW = 6


def b_spline_cubic(x, grid):
    dist = np.abs(x[..., None] - grid) / HSTEP
    inner = 2.0 / 3.0 - dist * dist + dist * dist * dist * 0.5
    t = 2.0 - dist
    outer = t * t * t / 6.0
    return np.where(dist < 1.0, inner, np.where(dist < 2.0, outer, 0.0))


def setup_inputs():
    wide = np.abs(np.log2(mx_kscale(K))).max() > 0.0
    x = f64(bf(np.random.standard_normal((B, I))))
    w = np.random.standard_normal((I, J, C)) * 1.5 / np.sqrt(I)
    grid = bf(np.linspace(-1.0, 1.0, C) + 0.2 * HSTEP * np.random.standard_normal(C))
    u = np.random.uniform(0.5, 1.0, (B, I))
    if wide:
        g = f64(grid)
        cs = np.argmin(np.abs(g - 2.0 * HSTEP))
        edge = g[cs] - 2.0 * HSTEP
        inside = (x > edge) & (x < edge + 4.0 * HSTEP)
        x = np.where(inside, edge + HSTEP * u * 2.0 ** -PW, x)
        w[:, :, cs] *= 2.0 ** (3 * PW + 3)
    return {"x": bf(x), "spline_weight": bf(w), "grid": grid}


def reference(x, spline_weight, grid):
    x_norm = np.clip(f64(x), -0.99, 0.99)
    basis = b_spline_cubic(x_norm, f64(grid))
    bk = basis.transpose(0, 2, 1).reshape(B, K)
    wk = f64(spline_weight).transpose(2, 0, 1).reshape(K, J)
    return mxq(bk, 1, "e4m3") @ mxq(wk, 0, "e4m3")

@@ -1,0 +1,211 @@
+import math
+from contextlib import ExitStack
+
+import concourse.mybir as mybir
+from concourse.masks import make_identity
+
+F32 = mybir.dt.float32
+BF16 = mybir.dt.bfloat16
+U32 = mybir.dt.uint32
+U8 = mybir.dt.uint8
+FP8X4 = mybir.dt.float8_e4m3fn_x4
+ALU = mybir.AluOpType
+ACT = mybir.ActivationFunctionType
+
+B, I, J, C = 8192, 32, 256, 32
+K = C * I
+FLOPS = 2 * B * K * J
+
+P = 128
+PACK = 4
+K_PASS = P * PACK
+PASSES = K // K_PASS
+KNOTS = K_PASS // I
+ROWS = I // PACK
+INV_H = (C - 1) / 2.0
+CLIP = 0.99
+
+N_PER_P = B // P
+TILES = 4
+CHUNKS = N_PER_P // TILES
+COLS = TILES * P * PACK
+WORDS = COLS // PACK
+
+
+def tile_fastkanlayer_pa_t_kernel(tc, x, spline_weight, grid, out):
+    nc = tc.nc
+    out_rows = out.rearrange("(p n) j -> p (n j)", n=N_PER_P)
+    scratch = out_rows[:, (N_PER_P * J - COLS) :]
+
+    with ExitStack() as ctx:
+        keep = ctx.enter_context(tc.tile_pool(name="keep", bufs=1))
+        psum_setup = ctx.enter_context(tc.psum_pool(name="psum_setup", bufs=2))
+        psum_acc = ctx.enter_context(tc.psum_pool(name="psum_acc", bufs=4))
+
+        neg_knot = keep.tile([P, PASSES], F32)
+        w_codes = keep.tile([P, PASSES, J], U32, align_bytes=64)
+        w_scales = keep.tile([P, PASSES, J], U8, align_bytes=64)
+
+        with tc.tile_pool(name="setup", bufs=1) as setup:
+            ident_f32 = setup.tile([P, P], F32)
+            make_identity(nc, ident_f32[:])
+            ident_bf16 = setup.tile([P, P], BF16)
+            make_identity(nc, ident_bf16[:])
+
+            x_rows = setup.tile([P, N_PER_P * I], BF16)
+            nc.sync.dma_start(out=x_rows[:], in_=x.rearrange("(p n) i -> p (n i)", n=N_PER_P))
+            x_by_tile = x_rows[:].rearrange(
+                "p (s g r t) -> p g t s r", s=CHUNKS, g=TILES, r=ROWS, t=PACK
+            )
+            x_clip = setup.tile([P, TILES, PACK, P], F32)
+            x_feat = setup.tile([P, TILES, P, PACK], F32)
+            for g in range(TILES):
+                nc.vector.tensor_scalar(
+                    out=x_clip[:, g].rearrange("p t (s r) -> p t s r", s=CHUNKS),
+                    in0=x_by_tile[:, g],
+                    scalar1=CLIP,
+                    scalar2=-CLIP,
+                    op0=ALU.min,
+                    op1=ALU.max,
+                )
+                x_t = psum_setup.tile([P, PACK, P], F32)
+                for t in range(PACK):
+                    nc.tensor.transpose(x_t[:, t, :], x_clip[:, g, t, :], ident_f32[:])
+                nc.vector.tensor_copy(out=x_feat[:, g], in_=x_t[:].rearrange("q t p -> q p t"))
+            nc.sync.dma_start(out=scratch, in_=x_feat[:].rearrange("q g p t -> q (g p t)"))
+
+            grid_rows = setup.tile([PASSES, KNOTS], BF16)
+            nc.scalar.dma_start(out=grid_rows[:], in_=grid.rearrange("(h c) -> h c", h=PASSES))
+            grid_wide = setup.tile([P, P], F32)
+            nc.vector.memset(grid_wide[:], 0.0)
+            nc.vector.tensor_copy(
+                out=grid_wide[0:PASSES, :].rearrange("h (c r) -> h c r", r=ROWS),
+                in_=grid_rows[:].unsqueeze(2).to_broadcast([PASSES, KNOTS, ROWS]),
+            )
+            grid_t = psum_setup.tile([P, PACK, P], F32, tag="x_t")
+            nc.tensor.transpose(grid_t[:, 0, :], grid_wide[:], ident_f32[:])
+            nc.vector.tensor_scalar_mul(out=neg_knot[:], in0=grid_t[:, 0, 0:PASSES], scalar1=-INV_H)
+
+            w_rows = setup.tile([P, I, J // P, C], BF16)
+            nc.scalar.dma_start(
+                out=w_rows[:], in_=spline_weight.rearrange("i (jh jl) c -> jl i jh c", jl=P)
+            )
+            w_by_pass = w_rows[:].rearrange("p (r t) jh (h c) -> p h jh t c r", t=PACK, h=PASSES)
+            w_sorted = setup.tile([P, PASSES, J // P, PACK, P], BF16)
+            w_grouped = setup.tile([P, PASSES, J, PACK], BF16, align_bytes=64)
+            for h in range(PASSES):
+                for jh in range(J // P):
+                    nc.vector.tensor_copy(
+                        out=w_sorted[:, h, jh].rearrange("p t (c r) -> p t c r", r=ROWS),
+                        in_=w_by_pass[:, h, jh],
+                    )
+                    w_t = psum_setup.tile([P, PACK, P], BF16)
+                    for t in range(PACK):
+                        nc.tensor.transpose(w_t[:, t, :], w_sorted[:, h, jh, t, :], ident_bf16[:])
+                    nc.vector.tensor_copy(
+                        out=w_grouped[:, h, jh * P : (jh + 1) * P, :],
+                        in_=w_t[:].rearrange("q t j -> q j t"),
+                    )
+            for h in range(PASSES):
+                nc.vector.quantize_mx(
+                    out=w_codes[:, h, :].bitcast(FP8X4),
+                    scales=w_scales[:, h, :],
+                    in_=w_grouped[:, h].rearrange("q j t -> q (j t)"),
+                )
+
+        x_pool = ctx.enter_context(tc.tile_pool(name="x_pool", bufs=3))
+        work = ctx.enter_context(tc.tile_pool(name="work", bufs=2))
+
+        def load_chunk(s):
+            x_rep = x_pool.tile([P, COLS], F32, name="x_rep")
+            for r in range(ROWS):
+                q = s * ROWS + r
+                nc.sync.dma_start(
+                    out=x_rep[r:P:ROWS, :], in_=scratch[q : q + 1, :].to_broadcast([KNOTS, COLS])
+                )
+            return x_rep
+
+        def powers(s, x_rep):
+            dist = work.tile([P, PASSES, COLS], F32, name="dist")
+            cube = work.tile([P, PASSES, COLS], F32, name="cube")
+            bowl = work.tile([P, PASSES, COLS], F32, name="bowl")
+            for h in range(PASSES):
+                nc.scalar.activation(
+                    out=dist[:, h], in_=x_rep[:], func=ACT.Abs, bias=neg_knot[:, h : h + 1], scale=INV_H
+                )
+            for h in range(PASSES):
+                nc.scalar.activation(
+                    out=cube[:, h], in_=dist[:, h], func=ACT.Square,
+                    bias=-2.0 / math.sqrt(6.0), scale=1.0 / math.sqrt(6.0),
+                )
+            for h in range(PASSES):
+                nc.scalar.activation(
+                    out=bowl[:, h], in_=dist[:, h], func=ACT.Square,
+                    bias=-1.5 * math.sqrt(2.0), scale=math.sqrt(2.0),
+                )
+            return dist, cube, bowl
+
+        def spline(dist, cube, bowl):
+            neg_basis = work.tile([P, PASSES, COLS], BF16, name="neg_basis")
+            basis = work.tile([P, PASSES, COLS], BF16, align_bytes=64, name="basis")
+            codes = work.tile([P, PASSES, WORDS], U32, align_bytes=64, name="codes")
+            scales = work.tile([P, PASSES, WORDS], U8, align_bytes=64, name="scales")
+            for h in range(PASSES):
+                nc.vector.scalar_tensor_tensor(
+                    out=cube[:, h], in0=dist[:, h], scalar=2.0, in1=cube[:, h],
+                    op0=ALU.subtract, op1=ALU.mult,
+                )
+            for h in range(PASSES):
+                nc.vector.scalar_tensor_tensor(
+                    out=bowl[:, h], in0=cube[:, h], scalar=-3.0, in1=bowl[:, h],
+                    op0=ALU.mult, op1=ALU.subtract,
+                )
+            for h in range(PASSES):
+                nc.vector.scalar_tensor_tensor(
+                    out=neg_basis[:, h], in0=bowl[:, h], scalar=1.0 / 6.0, in1=cube[:, h],
+                    op0=ALU.subtract, op1=ALU.max,
+                )
+            for h in range(PASSES):
+                nc.vector.tensor_scalar(
+                    out=basis[:, h], in0=neg_basis[:, h], scalar1=-1.0, scalar2=0.0,
+                    op0=ALU.mult, op1=ALU.max,
+                )
+            for h in range(PASSES):
+                nc.vector.quantize_mx(
+                    out=codes[:, h, :].bitcast(FP8X4), scales=scales[:, h, :], in_=basis[:, h]
+                )
+            return codes, scales
+
+        def multiply(s, codes, scales):
+            result = work.tile([P, TILES, J], F32, name="result")
+            for pair in range(TILES // 2):
+                acc = psum_acc.tile([P, 2, J], F32, name="acc")
+                for half in range(2):
+                    g = 2 * pair + half
+                    for h in range(PASSES):
+                        nc.tensor.matmul_mx(
+                            out=acc[:, half, :],
+                            lhsT=codes[:, h, g * P : (g + 1) * P].bitcast(FP8X4),
+                            lhsT_scale=scales[:, h, g * P : (g + 1) * P],
+                            rhs=w_codes[:, h, :].bitcast(FP8X4),
+                            rhs_scale=w_scales[:, h, :],
+                            start=(h == 0),
+                            stop=(h == PASSES - 1),
+                        )
+                nc.scalar.copy(out=result[:, 2 * pair : 2 * pair + 2, :], in_=acc[:])
+            nc.sync.dma_start(
+                out=out_rows[:, s * TILES * J : (s + 1) * TILES * J],
+                in_=result[:].rearrange("p g j -> p (g j)"),
+            )
+
+        with tc.manual_schedule():
+            x_reps = [load_chunk(0), load_chunk(1)]
+            squares = powers(0, x_reps[0])
+            for s in range(CHUNKS):
+                if s + 2 < CHUNKS:
+                    x_reps.append(load_chunk(s + 2))
+                ready = squares
+                if s + 1 < CHUNKS:
+                    squares = powers(s + 1, x_reps[s + 1])
+                codes, scales = spline(ready[0], ready[1], ready[2])
+                multiply(s, codes, scales)

@@ -136,7 +136,7 @@ def tile_fastkanlayer_pa_t_kernel(tc, x, spline_weight, grid, out):
             for h in range(PASSES):
                 nc.scalar.activation(
                     out=cube[:, h], in_=dist[:, h], func=ACT.Square,
-                    bias=-2.0 / math.sqrt(6.0), scale=1.0 / math.sqrt(6.0),
+                    bias=-2.0 / math.sqrt(2.0), scale=1.0 / math.sqrt(2.0),
                 )
             for h in range(PASSES):
                 nc.scalar.activation(
@@ -146,7 +146,8 @@ def tile_fastkanlayer_pa_t_kernel(tc, x, spline_weight, grid, out):
             return dist, cube, bowl
 
         def spline(dist, cube, bowl):
-            neg_basis = work.tile([P, PASSES, COLS], BF16, name="neg_basis")
+            outer = work.tile([P, PASSES, COLS], BF16, name="outer")
+            inner = work.tile([P, PASSES, COLS], BF16, name="inner")
             basis = work.tile([P, PASSES, COLS], BF16, align_bytes=64, name="basis")
             codes = work.tile([P, PASSES, WORDS], U32, align_bytes=64, name="codes")
             scales = work.tile([P, PASSES, WORDS], U8, align_bytes=64, name="scales")
@@ -156,20 +157,17 @@ def tile_fastkanlayer_pa_t_kernel(tc, x, spline_weight, grid, out):
                     op0=ALU.subtract, op1=ALU.mult,
                 )
             for h in range(PASSES):
-                nc.vector.scalar_tensor_tensor(
-                    out=bowl[:, h], in0=cube[:, h], scalar=-3.0, in1=bowl[:, h],
-                    op0=ALU.mult, op1=ALU.subtract,
-                )
-            for h in range(PASSES):
-                nc.vector.scalar_tensor_tensor(
-                    out=neg_basis[:, h], in0=bowl[:, h], scalar=1.0 / 6.0, in1=cube[:, h],
-                    op0=ALU.subtract, op1=ALU.max,
-                )
-            for h in range(PASSES):
                 nc.vector.tensor_scalar(
-                    out=basis[:, h], in0=neg_basis[:, h], scalar1=-1.0, scalar2=0.0,
+                    out=outer[:, h], in0=cube[:, h], scalar1=-1.0 / 3.0, scalar2=0.0,
                     op0=ALU.mult, op1=ALU.max,
                 )
+            for h in range(PASSES):
+                nc.vector.scalar_tensor_tensor(
+                    out=inner[:, h], in0=cube[:, h], scalar=1.0 / 6.0, in1=bowl[:, h],
+                    op0=ALU.add, op1=ALU.add,
+                )
+            for h in range(PASSES):
+                nc.vector.tensor_tensor(out=basis[:, h], in0=inner[:, h], in1=outer[:, h], op=ALU.min)
             for h in range(PASSES):
                 nc.vector.quantize_mx(
                     out=codes[:, h, :].bitcast(FP8X4), scales=scales[:, h, :], in_=basis[:, h]

@@ -28,7 +28,10 @@ CLIP = 0.99
 N_PER_P = B // P
 TILES = 4
 CHUNKS = N_PER_P // TILES
-COLS = TILES * P * PACK
+GROUPS = 4
+GROUP_CHUNKS = CHUNKS // GROUPS
+TILE_COLS = P * PACK
+COLS = TILES * TILE_COLS
 WORDS = COLS // PACK
 
 
@@ -39,99 +42,114 @@ def tile_fastkanlayer_pa_t_kernel(tc, x, spline_weight, grid, out):
 
     with ExitStack() as ctx:
         keep = ctx.enter_context(tc.tile_pool(name="keep", bufs=1))
+        x_pool = ctx.enter_context(tc.tile_pool(name="x_pool", bufs=3))
+        work = ctx.enter_context(tc.tile_pool(name="work", bufs=2))
         psum_setup = ctx.enter_context(tc.psum_pool(name="psum_setup", bufs=2))
         psum_acc = ctx.enter_context(tc.psum_pool(name="psum_acc", bufs=4))
 
-        neg_knot = keep.tile([P, PASSES], F32)
-        w_codes = keep.tile([P, PASSES, J], U32, align_bytes=64)
-        w_scales = keep.tile([P, PASSES, J], U8, align_bytes=64)
+        warm = keep.tile([P, 1], F32)
+        nc.vector.memset(warm[:], 0.0)
+        nc.scalar.activation(out=warm[:], in_=warm[:], func=ACT.Abs)
+        ident_f32 = keep.tile([P, P], F32)
+        make_identity(nc, ident_f32[:])
+        ident_bf16 = keep.tile([P, P], BF16)
+        make_identity(nc, ident_bf16[:])
 
-        with tc.tile_pool(name="setup", bufs=1) as setup:
-            ident_f32 = setup.tile([P, P], F32)
-            make_identity(nc, ident_f32[:])
-            ident_bf16 = setup.tile([P, P], BF16)
-            make_identity(nc, ident_bf16[:])
+        x_rows = keep.tile([P, GROUPS, GROUP_CHUNKS * TILES * I], BF16)
+        x_view = x.rearrange("(p a n) i -> p a (n i)", p=P, a=GROUPS)
+        for a in range(GROUPS):
+            nc.sync.dma_start(out=x_rows[:, a], in_=x_view[:, a])
+        grid_rows = keep.tile([PASSES, KNOTS], BF16)
+        nc.scalar.dma_start(out=grid_rows[:], in_=grid.rearrange("(h c) -> h c", h=PASSES))
+        w_rows = keep.tile([P, I, J // P, C], BF16)
+        nc.scalar.dma_start(
+            out=w_rows[:], in_=spline_weight.rearrange("i (jh jl) c -> jl i jh c", jl=P)
+        )
 
-            x_rows = setup.tile([P, N_PER_P * I], BF16)
-            nc.sync.dma_start(out=x_rows[:], in_=x.rearrange("(p n) i -> p (n i)", n=N_PER_P))
-            x_by_tile = x_rows[:].rearrange(
-                "p (s g r t) -> p g t s r", s=CHUNKS, g=TILES, r=ROWS, t=PACK
+        x_clip = keep.tile([P, GROUPS, PACK, P], F32)
+        x_feat = keep.tile([P, GROUPS, P, PACK], F32)
+
+        def prepare_group(a):
+            nc.vector.tensor_scalar(
+                out=x_clip[:, a].rearrange("p t (m r) -> p t m r", r=ROWS),
+                in0=x_rows[:, a].rearrange("p (m r t) -> p t m r", r=ROWS, t=PACK),
+                scalar1=CLIP,
+                scalar2=-CLIP,
+                op0=ALU.min,
+                op1=ALU.max,
             )
-            x_clip = setup.tile([P, TILES, PACK, P], F32)
-            x_feat = setup.tile([P, TILES, P, PACK], F32)
-            for g in range(TILES):
-                nc.vector.tensor_scalar(
-                    out=x_clip[:, g].rearrange("p t (s r) -> p t s r", s=CHUNKS),
-                    in0=x_by_tile[:, g],
-                    scalar1=CLIP,
-                    scalar2=-CLIP,
-                    op0=ALU.min,
-                    op1=ALU.max,
-                )
-                x_t = psum_setup.tile([P, PACK, P], F32)
-                for t in range(PACK):
-                    nc.tensor.transpose(x_t[:, t, :], x_clip[:, g, t, :], ident_f32[:])
-                nc.vector.tensor_copy(out=x_feat[:, g], in_=x_t[:].rearrange("q t p -> q p t"))
-            nc.sync.dma_start(out=scratch, in_=x_feat[:].rearrange("q g p t -> q (g p t)"))
-
-            grid_rows = setup.tile([PASSES, KNOTS], BF16)
-            nc.scalar.dma_start(out=grid_rows[:], in_=grid.rearrange("(h c) -> h c", h=PASSES))
-            grid_wide = setup.tile([P, P], F32)
-            nc.vector.memset(grid_wide[:], 0.0)
-            nc.vector.tensor_copy(
-                out=grid_wide[0:PASSES, :].rearrange("h (c r) -> h c r", r=ROWS),
-                in_=grid_rows[:].unsqueeze(2).to_broadcast([PASSES, KNOTS, ROWS]),
+            x_t = psum_setup.tile([P, PACK, P], F32, name="x_t")
+            for t in range(PACK):
+                nc.tensor.transpose(x_t[:, t, :], x_clip[:, a, t, :], ident_f32[:])
+            nc.vector.tensor_copy(out=x_feat[:, a], in_=x_t[:].rearrange("q t p -> q p t"))
+            nc.sync.dma_start(
+                out=scratch[:, a * TILE_COLS : (a + 1) * TILE_COLS],
+                in_=x_feat[:, a].rearrange("q p t -> q (p t)"),
             )
-            grid_t = psum_setup.tile([P, PACK, P], F32, tag="x_t")
-            nc.tensor.transpose(grid_t[:, 0, :], grid_wide[:], ident_f32[:])
-            nc.vector.tensor_scalar_mul(out=neg_knot[:], in0=grid_t[:, 0, 0:PASSES], scalar1=-INV_H)
-
-            w_rows = setup.tile([P, I, J // P, C], BF16)
-            nc.scalar.dma_start(
-                out=w_rows[:], in_=spline_weight.rearrange("i (jh jl) c -> jl i jh c", jl=P)
-            )
-            w_by_pass = w_rows[:].rearrange("p (r t) jh (h c) -> p h jh t c r", t=PACK, h=PASSES)
-            w_sorted = setup.tile([P, PASSES, J // P, PACK, P], BF16)
-            w_grouped = setup.tile([P, PASSES, J, PACK], BF16, align_bytes=64)
-            for h in range(PASSES):
-                for jh in range(J // P):
-                    nc.vector.tensor_copy(
-                        out=w_sorted[:, h, jh].rearrange("p t (c r) -> p t c r", r=ROWS),
-                        in_=w_by_pass[:, h, jh],
-                    )
-                    w_t = psum_setup.tile([P, PACK, P], BF16)
-                    for t in range(PACK):
-                        nc.tensor.transpose(w_t[:, t, :], w_sorted[:, h, jh, t, :], ident_bf16[:])
-                    nc.vector.tensor_copy(
-                        out=w_grouped[:, h, jh * P : (jh + 1) * P, :],
-                        in_=w_t[:].rearrange("q t j -> q j t"),
-                    )
-            for h in range(PASSES):
-                nc.vector.quantize_mx(
-                    out=w_codes[:, h, :].bitcast(FP8X4),
-                    scales=w_scales[:, h, :],
-                    in_=w_grouped[:, h].rearrange("q j t -> q (j t)"),
-                )
-
-        x_pool = ctx.enter_context(tc.tile_pool(name="x_pool", bufs=3))
-        work = ctx.enter_context(tc.tile_pool(name="work", bufs=2))
 
         def load_chunk(s):
-            x_rep = x_pool.tile([P, COLS], F32, name="x_rep")
+            x_rep = x_pool.tile([P, TILES, TILE_COLS], F32, name="x_rep")
+            a = s // GROUP_CHUNKS
+            first = (s % GROUP_CHUNKS) * TILES * ROWS
             for r in range(ROWS):
-                q = s * ROWS + r
+                rows_of_r = scratch[
+                    first + r : first + TILES * ROWS : ROWS, a * TILE_COLS : (a + 1) * TILE_COLS
+                ]
                 nc.sync.dma_start(
-                    out=x_rep[r:P:ROWS, :], in_=scratch[q : q + 1, :].to_broadcast([KNOTS, COLS])
+                    out=x_rep[r:P:ROWS],
+                    in_=rows_of_r.unsqueeze(0).to_broadcast([KNOTS, TILES, TILE_COLS]),
                 )
             return x_rep
 
-        def powers(s, x_rep):
+        prepare_group(0)
+        x_reps = [load_chunk(0), load_chunk(1)]
+
+        neg_knot = keep.tile([P, PASSES], F32)
+        grid_wide = keep.tile([P, P], F32)
+        nc.vector.memset(grid_wide[:], 0.0)
+        nc.vector.tensor_copy(
+            out=grid_wide[0:PASSES, :].rearrange("h (c r) -> h c r", r=ROWS),
+            in_=grid_rows[:].unsqueeze(2).to_broadcast([PASSES, KNOTS, ROWS]),
+        )
+        grid_t = psum_setup.tile([P, PACK, P], F32, tag="x_t")
+        nc.tensor.transpose(grid_t[:, 0, :], grid_wide[:], ident_f32[:])
+        nc.vector.tensor_scalar_mul(out=neg_knot[:], in0=grid_t[:, 0, 0:PASSES], scalar1=-INV_H)
+
+        for a in range(1, GROUPS):
+            prepare_group(a)
+
+        w_codes = keep.tile([P, PASSES, J], U32, align_bytes=64)
+        w_scales = keep.tile([P, PASSES, J], U8, align_bytes=64)
+        w_by_pass = w_rows[:].rearrange("p (r t) jh (h c) -> p h jh t c r", t=PACK, h=PASSES)
+        w_sorted = keep.tile([P, PASSES, J // P, PACK, P], BF16)
+        w_grouped = keep.tile([P, PASSES, J, PACK], BF16, align_bytes=64)
+        for h in range(PASSES):
+            for jh in range(J // P):
+                nc.vector.tensor_copy(
+                    out=w_sorted[:, h, jh].rearrange("p t (c r) -> p t c r", r=ROWS),
+                    in_=w_by_pass[:, h, jh],
+                )
+                w_t = psum_setup.tile([P, PACK, P], BF16)
+                for t in range(PACK):
+                    nc.tensor.transpose(w_t[:, t, :], w_sorted[:, h, jh, t, :], ident_bf16[:])
+                nc.vector.tensor_copy(
+                    out=w_grouped[:, h, jh * P : (jh + 1) * P, :],
+                    in_=w_t[:].rearrange("q t j -> q j t"),
+                )
+        for h in range(PASSES):
+            nc.vector.quantize_mx(
+                out=w_codes[:, h, :].bitcast(FP8X4),
+                scales=w_scales[:, h, :],
+                in_=w_grouped[:, h].rearrange("q j t -> q (j t)"),
+            )
+
+        def powers(x_rep):
             dist = work.tile([P, PASSES, COLS], F32, name="dist")
             cube = work.tile([P, PASSES, COLS], F32, name="cube")
             bowl = work.tile([P, PASSES, COLS], F32, name="bowl")
             for h in range(PASSES):
                 nc.scalar.activation(
-                    out=dist[:, h], in_=x_rep[:], func=ACT.Abs, bias=neg_knot[:, h : h + 1], scale=INV_H
+                    out=dist[:, h], in_=x_rep[:].rearrange("q g c -> q (g c)"), func=ACT.Abs, bias=neg_knot[:, h : h + 1], scale=INV_H
                 )
             for h in range(PASSES):
                 nc.scalar.activation(
@@ -197,13 +215,12 @@ def tile_fastkanlayer_pa_t_kernel(tc, x, spline_weight, grid, out):
             )
 
         with tc.manual_schedule():
-            x_reps = [load_chunk(0), load_chunk(1)]
-            squares = powers(0, x_reps[0])
+            squares = powers(x_reps[0])
             for s in range(CHUNKS):
                 if s + 2 < CHUNKS:
                     x_reps.append(load_chunk(s + 2))
                 ready = squares
                 if s + 1 < CHUNKS:
-                    squares = powers(s + 1, x_reps[s + 1])
+                    squares = powers(x_reps[s + 1])
                 codes, scales = spline(ready[0], ready[1], ready[2])
                 multiply(s, codes, scales)

@@ -66,6 +66,17 @@ def tile_fastkanlayer_pa_t_kernel(tc, x, spline_weight, grid, out):
             out=w_rows[:], in_=spline_weight.rearrange("i (jh jl) c -> jl i jh c", jl=P)
         )
 
+        neg_knot = keep.tile([P, PASSES], F32)
+        grid_wide = keep.tile([P, P], F32)
+        nc.vector.memset(grid_wide[:], 0.0)
+        nc.vector.tensor_copy(
+            out=grid_wide[0:PASSES, :].rearrange("h (c r) -> h c r", r=ROWS),
+            in_=grid_rows[:].unsqueeze(2).to_broadcast([PASSES, KNOTS, ROWS]),
+        )
+        grid_t = psum_setup.tile([P, PACK, P], F32, tag="x_t")
+        nc.tensor.transpose(grid_t[:, 0, :], grid_wide[:], ident_f32[:])
+        nc.vector.tensor_scalar_mul(out=neg_knot[:], in0=grid_t[:, 0, 0:PASSES], scalar1=-INV_H)
+
         x_clip = keep.tile([P, GROUPS, PACK, P], F32)
         x_feat = keep.tile([P, GROUPS, P, PACK], F32)
 
@@ -101,19 +112,27 @@ def tile_fastkanlayer_pa_t_kernel(tc, x, spline_weight, grid, out):
                 )
             return x_rep
 
-        prepare_group(0)
-        x_reps = [load_chunk(0), load_chunk(1)]
+        x_wide = keep.tile([P, TILES, PACK, P], F32)
+        x_first = []
+        for g in range(TILES):
+            nc.vector.tensor_scalar(
+                out=x_wide[:, g].rearrange("p t (c r) -> p t c r", r=ROWS),
+                in0=x_rows[:, 0, g * I : (g + 1) * I]
+                .rearrange("p (r t) -> p t r", t=PACK)
+                .unsqueeze(2)
+                .to_broadcast([P, PACK, KNOTS, ROWS]),
+                scalar1=CLIP,
+                scalar2=-CLIP,
+                op0=ALU.min,
+                op1=ALU.max,
+            )
+            x_wide_t = psum_acc.tile([P, PACK, P], F32, tag="acc")
+            for t in range(PACK):
+                nc.tensor.transpose(x_wide_t[:, t, :], x_wide[:, g, t, :], ident_f32[:])
+            x_first.append(x_wide_t[:].rearrange("q t p -> q p t"))
 
-        neg_knot = keep.tile([P, PASSES], F32)
-        grid_wide = keep.tile([P, P], F32)
-        nc.vector.memset(grid_wide[:], 0.0)
-        nc.vector.tensor_copy(
-            out=grid_wide[0:PASSES, :].rearrange("h (c r) -> h c r", r=ROWS),
-            in_=grid_rows[:].unsqueeze(2).to_broadcast([PASSES, KNOTS, ROWS]),
-        )
-        grid_t = psum_setup.tile([P, PACK, P], F32, tag="x_t")
-        nc.tensor.transpose(grid_t[:, 0, :], grid_wide[:], ident_f32[:])
-        nc.vector.tensor_scalar_mul(out=neg_knot[:], in0=grid_t[:, 0, 0:PASSES], scalar1=-INV_H)
+        prepare_group(0)
+        x_reps = {1: load_chunk(1)}
 
         for a in range(1, GROUPS):
             prepare_group(a)
@@ -143,14 +162,22 @@ def tile_fastkanlayer_pa_t_kernel(tc, x, spline_weight, grid, out):
                 in_=w_grouped[:, h].rearrange("q j t -> q (j t)"),
             )
 
-        def powers(x_rep):
+        def powers(x_parts):
             dist = work.tile([P, PASSES, COLS], F32, name="dist")
             cube = work.tile([P, PASSES, COLS], F32, name="cube")
             bowl = work.tile([P, PASSES, COLS], F32, name="bowl")
+            part_cols = COLS // len(x_parts)
             for h in range(PASSES):
-                nc.scalar.activation(
-                    out=dist[:, h], in_=x_rep[:].rearrange("q g c -> q (g c)"), func=ACT.Abs, bias=neg_knot[:, h : h + 1], scale=INV_H
-                )
+                for n, x_part in enumerate(x_parts):
+                    nc.scalar.activation(
+                        out=dist[:, h, n * part_cols : (n + 1) * part_cols].rearrange(
+                            "q (p t) -> q p t", t=PACK
+                        ),
+                        in_=x_part,
+                        func=ACT.Abs,
+                        bias=neg_knot[:, h : h + 1],
+                        scale=INV_H,
+                    )
             for h in range(PASSES):
                 nc.scalar.activation(
                     out=cube[:, h], in_=dist[:, h], func=ACT.Square,
@@ -209,18 +236,19 @@ def tile_fastkanlayer_pa_t_kernel(tc, x, spline_weight, grid, out):
                             stop=(h == PASSES - 1),
                         )
                 nc.scalar.copy(out=result[:, 2 * pair : 2 * pair + 2, :], in_=acc[:])
-            nc.sync.dma_start(
-                out=out_rows[:, s * TILES * J : (s + 1) * TILES * J],
-                in_=result[:].rearrange("p g j -> p (g j)"),
-            )
+                first_row = s * TILES + 2 * pair
+                nc.sync.dma_start(
+                    out=out_rows[:, first_row * J : (first_row + 2) * J],
+                    in_=result[:, 2 * pair : 2 * pair + 2, :].rearrange("p g j -> p (g j)"),
+                )
 
         with tc.manual_schedule():
-            squares = powers(x_reps[0])
+            squares = powers(x_first)
             for s in range(CHUNKS):
                 if s + 2 < CHUNKS:
-                    x_reps.append(load_chunk(s + 2))
+                    x_reps[s + 2] = load_chunk(s + 2)
                 ready = squares
                 if s + 1 < CHUNKS:
-                    squares = powers(x_reps[s + 1])
+                    squares = powers([x_reps[s + 1][:].rearrange("q g (p t) -> q (g p) t", t=PACK)])
                 codes, scales = spline(ready[0], ready[1], ready[2])
                 multiply(s, codes, scales)

@@ -1,4 +1,3 @@
-import math
 from contextlib import ExitStack
 
 import concourse.mybir as mybir
@@ -24,231 +23,268 @@ KNOTS = K_PASS // I
 ROWS = I // PACK
 INV_H = (C - 1) / 2.0
 CLIP = 0.99
-
 N_PER_P = B // P
-TILES = 4
-CHUNKS = N_PER_P // TILES
-GROUPS = 4
-GROUP_CHUNKS = CHUNKS // GROUPS
+PAIR = 2
 TILE_COLS = P * PACK
-COLS = TILES * TILE_COLS
-WORDS = COLS // PACK
+PAIR_COLS = PAIR * TILE_COLS
+
+CHUNKS = (4, 4, 8, 8, 8, 8, 8, 8, 4, 4)
+MAX_TILES = max(CHUNKS)
 
 
 def tile_fastkanlayer_pa_t_kernel(tc, x, spline_weight, grid, out):
     nc = tc.nc
     out_rows = out.rearrange("(p n) j -> p (n j)", n=N_PER_P)
-    scratch = out_rows[:, (N_PER_P * J - COLS) :]
+    x_view = x.rearrange("(p n) i -> p (n i)", n=N_PER_P)
 
     with ExitStack() as ctx:
         keep = ctx.enter_context(tc.tile_pool(name="keep", bufs=1))
-        x_pool = ctx.enter_context(tc.tile_pool(name="x_pool", bufs=3))
-        work = ctx.enter_context(tc.tile_pool(name="work", bufs=2))
-        psum_setup = ctx.enter_context(tc.psum_pool(name="psum_setup", bufs=2))
-        psum_acc = ctx.enter_context(tc.psum_pool(name="psum_acc", bufs=4))
+        dist_pool = ctx.enter_context(tc.tile_pool(name="dist_pool", bufs=3))
+        work = ctx.enter_context(tc.tile_pool(name="work", bufs=4))
+        psum_in = ctx.enter_context(tc.psum_pool(name="psum_in", bufs=4))
+        psum_two = ctx.enter_context(tc.psum_pool(name="psum_two", bufs=2))
+        ctx.enter_context(tc.manual_schedule())
 
         warm = keep.tile([P, 1], F32)
         nc.vector.memset(warm[:], 0.0)
+        grid_rows = keep.tile([P, C], BF16)
+        nc.sync.dma_start(out=grid_rows[:], in_=grid.partition_broadcast(P))
+        x_rows = keep.tile([P, N_PER_P * I], BF16)
+        x_splits = (0, 4 * I, 16 * I, N_PER_P * I)
+        for lo, hi in zip(x_splits[:-1], x_splits[1:]):
+            nc.sync.dma_start(out=x_rows[:, lo:hi], in_=x_view[:, lo:hi])
+        w_rows = keep.tile([P, I, J // P, C], BF16)
+        nc.scalar.dma_start(
+            out=w_rows[:], in_=spline_weight.rearrange("i (jh jl) c -> jl i jh c", jl=P)
+        )
         nc.scalar.activation(out=warm[:], in_=warm[:], func=ACT.Abs)
         ident_f32 = keep.tile([P, P], F32)
         make_identity(nc, ident_f32[:])
         ident_bf16 = keep.tile([P, P], BF16)
         make_identity(nc, ident_bf16[:])
 
-        x_rows = keep.tile([P, GROUPS, GROUP_CHUNKS * TILES * I], BF16)
-        x_view = x.rearrange("(p a n) i -> p a (n i)", p=P, a=GROUPS)
-        for a in range(GROUPS):
-            nc.sync.dma_start(out=x_rows[:, a], in_=x_view[:, a])
-        grid_rows = keep.tile([PASSES, KNOTS], BF16)
-        nc.scalar.dma_start(out=grid_rows[:], in_=grid.rearrange("(h c) -> h c", h=PASSES))
-        w_rows = keep.tile([P, I, J // P, C], BF16)
-        nc.scalar.dma_start(
-            out=w_rows[:], in_=spline_weight.rearrange("i (jh jl) c -> jl i jh c", jl=P)
-        )
-
-        neg_knot = keep.tile([P, PASSES], F32)
-        grid_wide = keep.tile([P, P], F32)
-        nc.vector.memset(grid_wide[:], 0.0)
-        nc.vector.tensor_copy(
-            out=grid_wide[0:PASSES, :].rearrange("h (c r) -> h c r", r=ROWS),
-            in_=grid_rows[:].unsqueeze(2).to_broadcast([PASSES, KNOTS, ROWS]),
-        )
-        grid_t = psum_setup.tile([P, PACK, P], F32, tag="x_t")
-        nc.tensor.transpose(grid_t[:, 0, :], grid_wide[:], ident_f32[:])
-        nc.vector.tensor_scalar_mul(out=neg_knot[:], in0=grid_t[:, 0, 0:PASSES], scalar1=-INV_H)
-
-        x_clip = keep.tile([P, GROUPS, PACK, P], F32)
-        x_feat = keep.tile([P, GROUPS, P, PACK], F32)
-
-        def prepare_group(a):
+        neg_knot = keep.tile([P, C], F32)
+        nc.vector.tensor_scalar_mul(out=neg_knot[:], in0=grid_rows[:], scalar1=-INV_H / 4.0)
+        x_clip = keep.tile([P, N_PER_P * I], F32)
+        for lo, hi in zip(x_splits[:-1], x_splits[1:]):
             nc.vector.tensor_scalar(
-                out=x_clip[:, a].rearrange("p t (m r) -> p t m r", r=ROWS),
-                in0=x_rows[:, a].rearrange("p (m r t) -> p t m r", r=ROWS, t=PACK),
-                scalar1=CLIP,
-                scalar2=-CLIP,
-                op0=ALU.min,
-                op1=ALU.max,
+                out=x_clip[:, lo:hi], in0=x_rows[:, lo:hi],
+                scalar1=CLIP, scalar2=-CLIP, op0=ALU.min, op1=ALU.max,
             )
-            x_t = psum_setup.tile([P, PACK, P], F32, name="x_t")
-            for t in range(PACK):
-                nc.tensor.transpose(x_t[:, t, :], x_clip[:, a, t, :], ident_f32[:])
-            nc.vector.tensor_copy(out=x_feat[:, a], in_=x_t[:].rearrange("q t p -> q p t"))
-            nc.sync.dma_start(
-                out=scratch[:, a * TILE_COLS : (a + 1) * TILE_COLS],
-                in_=x_feat[:, a].rearrange("q p t -> q (p t)"),
-            )
-
-        def load_chunk(s):
-            x_rep = x_pool.tile([P, TILES, TILE_COLS], F32, name="x_rep")
-            a = s // GROUP_CHUNKS
-            first = (s % GROUP_CHUNKS) * TILES * ROWS
-            for r in range(ROWS):
-                rows_of_r = scratch[
-                    first + r : first + TILES * ROWS : ROWS, a * TILE_COLS : (a + 1) * TILE_COLS
-                ]
-                nc.sync.dma_start(
-                    out=x_rep[r:P:ROWS],
-                    in_=rows_of_r.unsqueeze(0).to_broadcast([KNOTS, TILES, TILE_COLS]),
-                )
-            return x_rep
-
-        x_wide = keep.tile([P, TILES, PACK, P], F32)
-        x_first = []
-        for g in range(TILES):
-            nc.vector.tensor_scalar(
-                out=x_wide[:, g].rearrange("p t (c r) -> p t c r", r=ROWS),
-                in0=x_rows[:, 0, g * I : (g + 1) * I]
-                .rearrange("p (r t) -> p t r", t=PACK)
-                .unsqueeze(2)
-                .to_broadcast([P, PACK, KNOTS, ROWS]),
-                scalar1=CLIP,
-                scalar2=-CLIP,
-                op0=ALU.min,
-                op1=ALU.max,
-            )
-            x_wide_t = psum_acc.tile([P, PACK, P], F32, tag="acc")
-            for t in range(PACK):
-                nc.tensor.transpose(x_wide_t[:, t, :], x_wide[:, g, t, :], ident_f32[:])
-            x_first.append(x_wide_t[:].rearrange("q t p -> q p t"))
-
-        prepare_group(0)
-        x_reps = {1: load_chunk(1)}
-
-        for a in range(1, GROUPS):
-            prepare_group(a)
 
         w_codes = keep.tile([P, PASSES, J], U32, align_bytes=64)
         w_scales = keep.tile([P, PASSES, J], U8, align_bytes=64)
-        w_by_pass = w_rows[:].rearrange("p (r t) jh (h c) -> p h jh t c r", t=PACK, h=PASSES)
+        w_by_pass = w_rows[:].rearrange("p (t r) jh (h c) -> p h jh t c r", t=PACK, h=PASSES)
         w_sorted = keep.tile([P, PASSES, J // P, PACK, P], BF16)
         w_grouped = keep.tile([P, PASSES, J, PACK], BF16, align_bytes=64)
-        for h in range(PASSES):
-            for jh in range(J // P):
-                nc.vector.tensor_copy(
-                    out=w_sorted[:, h, jh].rearrange("p t (c r) -> p t c r", r=ROWS),
-                    in_=w_by_pass[:, h, jh],
-                )
-                w_t = psum_setup.tile([P, PACK, P], BF16)
-                for t in range(PACK):
-                    nc.tensor.transpose(w_t[:, t, :], w_sorted[:, h, jh, t, :], ident_bf16[:])
-                nc.vector.tensor_copy(
-                    out=w_grouped[:, h, jh * P : (jh + 1) * P, :],
-                    in_=w_t[:].rearrange("q t j -> q j t"),
-                )
-        for h in range(PASSES):
-            nc.vector.quantize_mx(
-                out=w_codes[:, h, :].bitcast(FP8X4),
-                scales=w_scales[:, h, :],
-                in_=w_grouped[:, h].rearrange("q j t -> q (j t)"),
-            )
 
-        def powers(x_parts):
-            dist = work.tile([P, PASSES, COLS], F32, name="dist")
-            cube = work.tile([P, PASSES, COLS], F32, name="cube")
-            bowl = work.tile([P, PASSES, COLS], F32, name="bowl")
-            part_cols = COLS // len(x_parts)
+        def prepare_weight():
             for h in range(PASSES):
-                for n, x_part in enumerate(x_parts):
-                    nc.scalar.activation(
-                        out=dist[:, h, n * part_cols : (n + 1) * part_cols].rearrange(
-                            "q (p t) -> q p t", t=PACK
-                        ),
-                        in_=x_part,
-                        func=ACT.Abs,
-                        bias=neg_knot[:, h : h + 1],
-                        scale=INV_H,
+                for jh in range(J // P):
+                    nc.vector.tensor_copy(
+                        out=w_sorted[:, h, jh].rearrange("p t (c r) -> p t c r", r=ROWS),
+                        in_=w_by_pass[:, h, jh],
                     )
             for h in range(PASSES):
-                nc.scalar.activation(
-                    out=cube[:, h], in_=dist[:, h], func=ACT.Square,
-                    bias=-2.0 / math.sqrt(2.0), scale=1.0 / math.sqrt(2.0),
-                )
-            for h in range(PASSES):
-                nc.scalar.activation(
-                    out=bowl[:, h], in_=dist[:, h], func=ACT.Square,
-                    bias=-1.5 * math.sqrt(2.0), scale=math.sqrt(2.0),
-                )
-            return dist, cube, bowl
-
-        def spline(dist, cube, bowl):
-            outer = work.tile([P, PASSES, COLS], BF16, name="outer")
-            inner = work.tile([P, PASSES, COLS], BF16, name="inner")
-            basis = work.tile([P, PASSES, COLS], BF16, align_bytes=64, name="basis")
-            codes = work.tile([P, PASSES, WORDS], U32, align_bytes=64, name="codes")
-            scales = work.tile([P, PASSES, WORDS], U8, align_bytes=64, name="scales")
-            for h in range(PASSES):
-                nc.vector.scalar_tensor_tensor(
-                    out=cube[:, h], in0=dist[:, h], scalar=2.0, in1=cube[:, h],
-                    op0=ALU.subtract, op1=ALU.mult,
-                )
-            for h in range(PASSES):
-                nc.vector.tensor_scalar(
-                    out=outer[:, h], in0=cube[:, h], scalar1=-1.0 / 3.0, scalar2=0.0,
-                    op0=ALU.mult, op1=ALU.max,
-                )
-            for h in range(PASSES):
-                nc.vector.scalar_tensor_tensor(
-                    out=inner[:, h], in0=cube[:, h], scalar=1.0 / 6.0, in1=bowl[:, h],
-                    op0=ALU.add, op1=ALU.add,
-                )
-            for h in range(PASSES):
-                nc.vector.tensor_tensor(out=basis[:, h], in0=inner[:, h], in1=outer[:, h], op=ALU.min)
+                for jh in range(J // P):
+                    w_t = psum_in.tile([P, PACK, P], BF16, tag="inner")
+                    for t in range(PACK):
+                        nc.tensor.transpose(w_t[:, t, :], w_sorted[:, h, jh, t, :], ident_bf16[:])
+                    nc.vector.tensor_copy(
+                        out=w_grouped[:, h, jh * P : (jh + 1) * P, :],
+                        in_=w_t[:].rearrange("q t j -> q j t"),
+                    )
             for h in range(PASSES):
                 nc.vector.quantize_mx(
-                    out=codes[:, h, :].bitcast(FP8X4), scales=scales[:, h, :], in_=basis[:, h]
+                    out=w_codes[:, h, :].bitcast(FP8X4),
+                    scales=w_scales[:, h, :],
+                    in_=w_grouped[:, h].rearrange("q j t -> q (j t)"),
                 )
-            return codes, scales
 
-        def multiply(s, codes, scales):
-            result = work.tile([P, TILES, J], F32, name="result")
-            for pair in range(TILES // 2):
-                acc = psum_acc.tile([P, 2, J], F32, name="acc")
-                for half in range(2):
-                    g = 2 * pair + half
-                    for h in range(PASSES):
-                        nc.tensor.matmul_mx(
-                            out=acc[:, half, :],
-                            lhsT=codes[:, h, g * P : (g + 1) * P].bitcast(FP8X4),
-                            lhsT_scale=scales[:, h, g * P : (g + 1) * P],
-                            rhs=w_codes[:, h, :].bitcast(FP8X4),
-                            rhs_scale=w_scales[:, h, :],
-                            start=(h == 0),
-                            stop=(h == PASSES - 1),
+        units = []
+        first_tile = 0
+        for tiles in CHUNKS:
+            for h in range(PASSES):
+                units.append((first_tile, tiles, h))
+            first_tile += tiles
+        steps = []
+        for u in range(len(units)):
+            for j in range(units[u][1] // PAIR):
+                steps.append((u, j))
+        n_steps = len(steps)
+
+        dists = {}
+        quads = {}
+        cubes = {}
+        outer_rows = {}
+        inners = {}
+        outers = {}
+        bases = {}
+        codes = {}
+        scales = {}
+
+        def distance(u, c):
+            first, tiles, h = units[u]
+            if u not in dists:
+                dist_u = dist_pool.tile([P, MAX_TILES, PACK, KNOTS, ROWS], F32, name="dist_u")
+                dists[u] = dist_u
+            nc.scalar.activation(
+                out=dists[u][:, 0:tiles, :, c, :],
+                in_=x_clip[:, first * I : (first + tiles) * I].rearrange(
+                    "p (a t r) -> p a t r", t=PACK, r=ROWS
+                ),
+                func=ACT.Abs,
+                bias=neg_knot[:, h * KNOTS + c : h * KNOTS + c + 1],
+                scale=INV_H / 4.0,
+            )
+
+        def dist_cols(k):
+            u, j = steps[k]
+            return dists[u][:, j * PAIR : (j + 1) * PAIR].rearrange("p a t c r -> p (a t c r)")
+
+        def square(k):
+            quad = work.tile([P, PAIR_COLS], F32, name="quad")
+            nc.scalar.activation(out=quad[:], in_=dist_cols(k), func=ACT.Square, bias=-1.0, scale=2.0)
+            quads[k] = quad
+
+        def multiply_cube(k):
+            cube = work.tile([P, PAIR_COLS], F32, name="cube")
+            nc.vector.scalar_tensor_tensor(
+                out=cube[:], in0=dist_cols(k), scalar=0.5, in1=quads[k][:],
+                op0=ALU.subtract, op1=ALU.mult,
+            )
+            cubes[k] = cube
+
+        def clip_outer(k):
+            outer_row = work.tile([P, PAIR * 2, P, 2], BF16, name="outer_row")
+            nc.vector.tensor_scalar(
+                out=outer_row[:],
+                in0=cubes[k][:].rearrange("p (au e m) -> p au m e", e=2, m=P),
+                scalar1=-1.0 / 3.0, scalar2=0.0, op0=ALU.mult, op1=ALU.max,
+            )
+            outer_rows[k] = outer_row
+
+        def transposes(k):
+            words = outer_rows[k][:].rearrange("p au m e -> p (au m e)").bitcast(F32)
+            outer_t = psum_two.tile([P, PAIR, 2, P], F32, name="outer_t")
+            for a in range(PAIR):
+                for w in range(2):
+                    at = (a * 2 + w) * P
+                    nc.tensor.transpose(outer_t[:, a, w, :], words[:, at : at + P], ident_f32[:])
+            outers[k] = outer_t
+            parts = (dist_cols(k), quads[k][:], cubes[k][:])
+            inners[k] = []
+            for a in range(PAIR):
+                inner_t = psum_in.tile([P, PACK, P], F32, tag="inner")
+                for t in range(PACK):
+                    at = (a * PACK + t) * P
+                    for n, part in enumerate(parts):
+                        nc.tensor.matmul(
+                            inner_t[:, t, :], part[:, at : at + P], ident_f32[:],
+                            start=(n == 0), stop=(n == len(parts) - 1), is_transpose=True,
                         )
-                nc.scalar.copy(out=result[:, 2 * pair : 2 * pair + 2, :], in_=acc[:])
-                first_row = s * TILES + 2 * pair
-                nc.sync.dma_start(
-                    out=out_rows[:, first_row * J : (first_row + 2) * J],
-                    in_=result[:, 2 * pair : 2 * pair + 2, :].rearrange("p g j -> p (g j)"),
-                )
+                inners[k].append(inner_t)
 
-        with tc.manual_schedule():
-            squares = powers(x_first)
-            for s in range(CHUNKS):
-                if s + 2 < CHUNKS:
-                    x_reps[s + 2] = load_chunk(s + 2)
-                ready = squares
-                if s + 1 < CHUNKS:
-                    squares = powers([x_reps[s + 1][:].rearrange("q g (p t) -> q (g p) t", t=PACK)])
-                codes, scales = spline(ready[0], ready[1], ready[2])
-                multiply(s, codes, scales)
+        def copy_outer(k):
+            outer_k = work.tile([P, PAIR, P, PACK], BF16, name="outer_k")
+            nc.scalar.copy(
+                out=outer_k[:].rearrange("q a p t -> q (a p t)").bitcast(F32).rearrange(
+                    "q (a p w) -> q a p w", a=PAIR, w=2
+                ),
+                in_=outers[k][:].rearrange("q a w p -> q a p w"),
+            )
+            outers[k] = outer_k
+
+        def minimum(k):
+            basis = work.tile([P, PAIR, P, PACK], BF16, align_bytes=64, name="basis")
+            for a in range(PAIR):
+                nc.vector.scalar_tensor_tensor(
+                    out=basis[:, a], in0=inners[k][a][:].rearrange("q t p -> q p t"),
+                    scalar=-5.0 / 12.0, in1=outers[k][:, a], op0=ALU.add, op1=ALU.min,
+                )
+            bases[k] = basis
+
+        def quantise(k):
+            u, j = steps[k]
+            first, tiles, h = units[u]
+            if h == 0 and j == 0:
+                code = work.tile([P, PASSES, MAX_TILES, P], U32, align_bytes=64, name="code")
+                scale = work.tile([P, PASSES, MAX_TILES, P], U8, align_bytes=64, name="scale")
+                codes[first] = code
+                scales[first] = scale
+            nc.vector.quantize_mx(
+                out=codes[first][:, h, j * PAIR : (j + 1) * PAIR].rearrange("q a p -> q (a p)").bitcast(FP8X4),
+                scales=scales[first][:, h, j * PAIR : (j + 1) * PAIR].rearrange("q a p -> q (a p)"),
+                in_=bases[k][:].rearrange("q a p t -> q (a p t)"),
+            )
+
+        ready = []
+        done = []
+
+        def multiply():
+            first, j = ready.pop(0)
+            acc = psum_two.tile([P, PAIR, J], F32, name="acc")
+            for a in range(PAIR):
+                for h in range(PASSES):
+                    nc.tensor.matmul_mx(
+                        out=acc[:, a, :],
+                        lhsT=codes[first][:, h, j * PAIR + a, :].bitcast(FP8X4),
+                        lhsT_scale=scales[first][:, h, j * PAIR + a, :],
+                        rhs=w_codes[:, h, :].bitcast(FP8X4),
+                        rhs_scale=w_scales[:, h, :],
+                        start=(h == 0),
+                        stop=(h == PASSES - 1),
+                    )
+            done.append((acc, first + j * PAIR))
+
+        def store():
+            acc, row = done.pop(0)
+            result = work.tile([P, PAIR * J], F32, name="result")
+            nc.scalar.activation(
+                out=result[:], in_=acc[:].rearrange("p a j -> p (a j)"), func=ACT.Copy, scale=8.0
+            )
+            nc.sync.dma_start(out=out_rows[:, row * J : (row + PAIR) * J], in_=result[:])
+
+        for c in range(KNOTS):
+            distance(0, c)
+        prepare_weight()
+
+        pending = []
+        for u in range(1, len(units)):
+            for c in range(KNOTS):
+                pending.append((u, c))
+        tick = 0
+        for k in range(-2, n_steps + 2):
+            if 0 <= k < n_steps:
+                transposes(k)
+            if 0 <= k + 2 < n_steps:
+                square(k + 2)
+            if 0 <= k + 1 < n_steps:
+                multiply_cube(k + 1)
+            if 0 <= k - 1 < n_steps:
+                quantise(k - 1)
+                u, j = steps[k - 1]
+                if units[u][2] == PASSES - 1:
+                    ready.append((units[u][0], j))
+            if 0 <= k < n_steps:
+                copy_outer(k)
+            if 0 <= k + 1 < n_steps:
+                clip_outer(k + 1)
+            while done:
+                store()
+            if 0 <= k + 2 < n_steps:
+                u, j = steps[k + 2]
+                unit_steps = units[u][1] // PAIR
+                for n in range(KNOTS // unit_steps):
+                    if pending:
+                        unit_c, c = pending.pop(0)
+                        distance(unit_c, c)
+            if 0 <= k < n_steps:
+                minimum(k)
+            tick += 1
+            if ready and (tick % 2 == 0 or len(ready) > 4 or k >= n_steps - 4):
+                multiply()
+        while ready:
+            multiply()
+        while done:
+            store()

@@ -54,7 +54,7 @@ def tile_fastkanlayer_pa_t_kernel(tc, x, spline_weight, grid, out):
         for lo, hi in zip(x_splits[:-1], x_splits[1:]):
             nc.sync.dma_start(out=x_rows[:, lo:hi], in_=x_view[:, lo:hi])
         w_rows = keep.tile([P, I, J // P, C], BF16)
-        nc.scalar.dma_start(
+        nc.sync.dma_start(
             out=w_rows[:], in_=spline_weight.rearrange("i (jh jl) c -> jl i jh c", jl=P)
         )
         nc.scalar.activation(out=warm[:], in_=warm[:], func=ACT.Abs)
@@ -78,28 +78,32 @@ def tile_fastkanlayer_pa_t_kernel(tc, x, spline_weight, grid, out):
         w_sorted = keep.tile([P, PASSES, J // P, PACK, P], BF16)
         w_grouped = keep.tile([P, PASSES, J, PACK], BF16, align_bytes=64)
 
-        def prepare_weight():
+        def sort_weight():
             for h in range(PASSES):
                 for jh in range(J // P):
-                    nc.vector.tensor_copy(
-                        out=w_sorted[:, h, jh].rearrange("p t (c r) -> p t c r", r=ROWS),
-                        in_=w_by_pass[:, h, jh],
-                    )
-            for h in range(PASSES):
-                for jh in range(J // P):
-                    w_t = psum_in.tile([P, PACK, P], BF16, tag="inner")
                     for t in range(PACK):
-                        nc.tensor.transpose(w_t[:, t, :], w_sorted[:, h, jh, t, :], ident_bf16[:])
-                    nc.vector.tensor_copy(
-                        out=w_grouped[:, h, jh * P : (jh + 1) * P, :],
-                        in_=w_t[:].rearrange("q t j -> q j t"),
-                    )
-            for h in range(PASSES):
-                nc.vector.quantize_mx(
-                    out=w_codes[:, h, :].bitcast(FP8X4),
-                    scales=w_scales[:, h, :],
-                    in_=w_grouped[:, h].rearrange("q j t -> q (j t)"),
+                        nc.gpsimd.tensor_scalar(
+                            out=w_sorted[:, h, jh, t].rearrange("p (c r) -> p c r", r=ROWS),
+                            in0=w_by_pass[:, h, jh, t],
+                            scalar1=1.0, scalar2=0.0, op0=ALU.mult, op1=ALU.add,
+                        )
+
+        def turn_weight(h):
+            for jh in range(J // P):
+                w_t = psum_in.tile([P, PACK, P], BF16, tag="inner")
+                for t in range(PACK):
+                    nc.tensor.transpose(w_t[:, t, :], w_sorted[:, h, jh, t, :], ident_bf16[:])
+                nc.scalar.copy(
+                    out=w_grouped[:, h, jh * P : (jh + 1) * P, :],
+                    in_=w_t[:].rearrange("q t j -> q j t"),
                 )
+
+        def quantise_weight(h):
+            nc.vector.quantize_mx(
+                out=w_codes[:, h, :].bitcast(FP8X4),
+                scales=w_scales[:, h, :],
+                in_=w_grouped[:, h].rearrange("q j t -> q (j t)"),
+            )
 
         units = []
         first_tile = 0
@@ -218,12 +222,18 @@ def tile_fastkanlayer_pa_t_kernel(tc, x, spline_weight, grid, out):
                 in_=bases[k][:].rearrange("q a p t -> q (a p t)"),
             )
 
+        twice = []
         ready = []
         done = []
 
+        half = []
+
         def multiply():
-            first, j = ready.pop(0)
-            acc = psum_two.tile([P, PAIR, J], F32, name="acc")
+            first, j = ready[0]
+            if not half:
+                acc = psum_two.tile([P, PAIR, J], F32, name="acc")
+                half.append(acc)
+            acc = half[0]
             for a in range(PAIR):
                 for h in range(PASSES):
                     nc.tensor.matmul_mx(
@@ -235,7 +245,12 @@ def tile_fastkanlayer_pa_t_kernel(tc, x, spline_weight, grid, out):
                         start=(h == 0),
                         stop=(h == PASSES - 1),
                     )
-            done.append((acc, first + j * PAIR))
+            twice.append(first)
+            if len(twice) == 2 or len(ready) > 4:
+                done.append((acc, first + j * PAIR))
+                ready.pop(0)
+                half.clear()
+                twice.clear()
 
         def store():
             acc, row = done.pop(0)
@@ -247,13 +262,12 @@ def tile_fastkanlayer_pa_t_kernel(tc, x, spline_weight, grid, out):
 
         for c in range(KNOTS):
             distance(0, c)
-        prepare_weight()
+        sort_weight()
 
         pending = []
         for u in range(1, len(units)):
             for c in range(KNOTS):
                 pending.append((u, c))
-        tick = 0
         for k in range(-2, n_steps + 2):
             if 0 <= k < n_steps:
                 transposes(k)
@@ -268,6 +282,10 @@ def tile_fastkanlayer_pa_t_kernel(tc, x, spline_weight, grid, out):
                     ready.append((units[u][0], j))
             if 0 <= k < n_steps:
                 copy_outer(k)
+            if 0 <= k < PASSES:
+                turn_weight(k)
+            if 0 <= k - 1 < PASSES:
+                quantise_weight(k - 1)
             if 0 <= k + 1 < n_steps:
                 clip_outer(k + 1)
             while done:
@@ -281,8 +299,7 @@ def tile_fastkanlayer_pa_t_kernel(tc, x, spline_weight, grid, out):
                         distance(unit_c, c)
             if 0 <= k < n_steps:
                 minimum(k)
-            tick += 1
-            if ready and (tick % 2 == 0 or len(ready) > 4 or k >= n_steps - 4):
+            if ready:
                 multiply()
         while ready:
             multiply()

@@ -268,13 +268,13 @@ def tile_fastkanlayer_pa_t_kernel(tc, x, spline_weight, grid, out):
         for u in range(1, len(units)):
             for c in range(KNOTS):
                 pending.append((u, c))
-        for k in range(-2, n_steps + 2):
-            if 0 <= k < n_steps:
-                transposes(k)
-            if 0 <= k + 2 < n_steps:
-                square(k + 2)
+        for k in range(-3, n_steps + 2):
             if 0 <= k + 1 < n_steps:
-                multiply_cube(k + 1)
+                transposes(k + 1)
+            if 0 <= k + 3 < n_steps:
+                square(k + 3)
+            if 0 <= k + 2 < n_steps:
+                multiply_cube(k + 2)
             if 0 <= k - 1 < n_steps:
                 quantise(k - 1)
                 u, j = steps[k - 1]
@@ -286,12 +286,12 @@ def tile_fastkanlayer_pa_t_kernel(tc, x, spline_weight, grid, out):
                 turn_weight(k)
             if 0 <= k - 1 < PASSES:
                 quantise_weight(k - 1)
-            if 0 <= k + 1 < n_steps:
-                clip_outer(k + 1)
+            if 0 <= k + 2 < n_steps:
+                clip_outer(k + 2)
             while done:
                 store()
-            if 0 <= k + 2 < n_steps:
-                u, j = steps[k + 2]
+            if 0 <= k + 3 < n_steps:
+                u, j = steps[k + 3]
                 unit_steps = units[u][1] // PAIR
                 for n in range(KNOTS // unit_steps):
                     if pending:

@@ -27,6 +27,8 @@ N_PER_P = B // P
 PAIR = 2
 TILE_COLS = P * PACK
 PAIR_COLS = PAIR * TILE_COLS
+UNFED_STEPS = 5
+UNFED_FILLS = 3
 
 CHUNKS = (4, 4, 8, 8, 8, 8, 8, 8, 4, 4)
 MAX_TILES = max(CHUNKS)
@@ -168,6 +170,12 @@ def tile_fastkanlayer_pa_t_kernel(tc, x, spline_weight, grid, out):
             )
             outer_rows[k] = outer_row
 
+        def wake():
+            busy = psum_in.tile([P, PACK * P], F32, tag="inner")
+            nc.tensor.matmul(
+                busy[:], ident_f32[:], dist_cols(0)[:, 0 : PACK * P], start=True, stop=True
+            )
+
         def transposes(k):
             words = outer_rows[k][:].rearrange("p au m e -> p (au m e)").bitcast(F32)
             outer_t = psum_two.tile([P, PAIR, 2, P], F32, name="outer_t")
@@ -180,6 +188,8 @@ def tile_fastkanlayer_pa_t_kernel(tc, x, spline_weight, grid, out):
             inners[k] = []
             for a in range(PAIR):
                 inner_t = psum_in.tile([P, PACK, P], F32, tag="inner")
+                for n in range(0 if a == 0 else UNFED_FILLS if k < UNFED_STEPS else 1):
+                    nc.tensor.matmul(inner_t[:, n, :], ident_f32[:], ident_f32[:], start=True, stop=True)
                 for t in range(PACK):
                     at = (a * PACK + t) * P
                     for n, part in enumerate(parts):
@@ -222,18 +232,12 @@ def tile_fastkanlayer_pa_t_kernel(tc, x, spline_weight, grid, out):
                 in_=bases[k][:].rearrange("q a p t -> q (a p t)"),
             )
 
-        twice = []
         ready = []
         done = []
 
-        half = []
-
         def multiply():
-            first, j = ready[0]
-            if not half:
-                acc = psum_two.tile([P, PAIR, J], F32, name="acc")
-                half.append(acc)
-            acc = half[0]
+            first, j = ready.pop(0)
+            acc = psum_two.tile([P, PAIR, J], F32, name="acc")
             for a in range(PAIR):
                 for h in range(PASSES):
                     nc.tensor.matmul_mx(
@@ -245,12 +249,7 @@ def tile_fastkanlayer_pa_t_kernel(tc, x, spline_weight, grid, out):
                         start=(h == 0),
                         stop=(h == PASSES - 1),
                     )
-            twice.append(first)
-            if len(twice) == 2 or len(ready) > 4:
-                done.append((acc, first + j * PAIR))
-                ready.pop(0)
-                half.clear()
-                twice.clear()
+            done.append((acc, first + j * PAIR))
 
         def store():
             acc, row = done.pop(0)
@@ -263,6 +262,7 @@ def tile_fastkanlayer_pa_t_kernel(tc, x, spline_weight, grid, out):
         for c in range(KNOTS):
             distance(0, c)
         sort_weight()
+        wake()
 
         pending = []
         for u in range(1, len(units)):
@@ -288,8 +288,6 @@ def tile_fastkanlayer_pa_t_kernel(tc, x, spline_weight, grid, out):
                 quantise_weight(k - 1)
             if 0 <= k + 2 < n_steps:
                 clip_outer(k + 2)
-            while done:
-                store()
             if 0 <= k + 3 < n_steps:
                 u, j = steps[k + 3]
                 unit_steps = units[u][1] // PAIR
@@ -297,9 +295,11 @@ def tile_fastkanlayer_pa_t_kernel(tc, x, spline_weight, grid, out):
                     if pending:
                         unit_c, c = pending.pop(0)
                         distance(unit_c, c)
+            while done:
+                store()
             if 0 <= k < n_steps:
                 minimum(k)
-            if ready:
+            if ready and (k % 2 == 0 or k >= n_steps - 4):
                 multiply()
         while ready:
             multiply()

@@ -26,12 +26,12 @@ CLIP = 0.99
 N_PER_P = B // P
 PAIR = 2
 TILE_COLS = P * PACK
-PAIR_COLS = PAIR * TILE_COLS
 UNFED_STEPS = 5
 UNFED_FILLS = 3
 
-CHUNKS = (4, 4, 8, 8, 8, 8, 8, 8, 4, 4)
+CHUNKS = (2, 2, 4, 8, 8, 8, 8, 8, 8, 4, 4)
 MAX_TILES = max(CHUNKS)
+STEP_TILES = 4
 
 
 def tile_fastkanlayer_pa_t_kernel(tc, x, spline_weight, grid, out):
@@ -41,8 +41,8 @@ def tile_fastkanlayer_pa_t_kernel(tc, x, spline_weight, grid, out):
 
     with ExitStack() as ctx:
         keep = ctx.enter_context(tc.tile_pool(name="keep", bufs=1))
-        dist_pool = ctx.enter_context(tc.tile_pool(name="dist_pool", bufs=3))
-        work = ctx.enter_context(tc.tile_pool(name="work", bufs=4))
+        dist_pool = ctx.enter_context(tc.tile_pool(name="dist_pool", bufs=4))
+        work = ctx.enter_context(tc.tile_pool(name="work", bufs=3))
         psum_in = ctx.enter_context(tc.psum_pool(name="psum_in", bufs=4))
         psum_two = ctx.enter_context(tc.psum_pool(name="psum_two", bufs=2))
         ctx.enter_context(tc.manual_schedule())
@@ -80,15 +80,12 @@ def tile_fastkanlayer_pa_t_kernel(tc, x, spline_weight, grid, out):
         w_sorted = keep.tile([P, PASSES, J // P, PACK, P], BF16)
         w_grouped = keep.tile([P, PASSES, J, PACK], BF16, align_bytes=64)
 
-        def sort_weight():
-            for h in range(PASSES):
-                for jh in range(J // P):
-                    for t in range(PACK):
-                        nc.gpsimd.tensor_scalar(
-                            out=w_sorted[:, h, jh, t].rearrange("p (c r) -> p c r", r=ROWS),
-                            in0=w_by_pass[:, h, jh, t],
-                            scalar1=1.0, scalar2=0.0, op0=ALU.mult, op1=ALU.add,
-                        )
+        def sort_weight(h):
+            for jh in range(J // P):
+                nc.vector.tensor_copy(
+                    out=w_sorted[:, h, jh].rearrange("p t (c r) -> p t c r", r=ROWS),
+                    in_=w_by_pass[:, h, jh],
+                )
 
         def turn_weight(h):
             for jh in range(J // P):
@@ -115,8 +112,10 @@ def tile_fastkanlayer_pa_t_kernel(tc, x, spline_weight, grid, out):
             first_tile += tiles
         steps = []
         for u in range(len(units)):
-            for j in range(units[u][1] // PAIR):
-                steps.append((u, j))
+            tiles_of_u = units[u][1]
+            step = STEP_TILES if tiles_of_u == MAX_TILES else PAIR
+            for at in range(0, tiles_of_u, step):
+                steps.append((u, at, step))
         n_steps = len(steps)
 
         dists = {}
@@ -145,27 +144,27 @@ def tile_fastkanlayer_pa_t_kernel(tc, x, spline_weight, grid, out):
             )
 
         def dist_cols(k):
-            u, j = steps[k]
-            return dists[u][:, j * PAIR : (j + 1) * PAIR].rearrange("p a t c r -> p (a t c r)")
+            u, at, tiles = steps[k]
+            return dists[u][:, at : at + tiles].rearrange("p a t c r -> p (a t c r)")
 
         def square(k):
-            quad = work.tile([P, PAIR_COLS], F32, name="quad")
-            nc.scalar.activation(out=quad[:], in_=dist_cols(k), func=ACT.Square, bias=-1.0, scale=2.0)
-            quads[k] = quad
+            quad = dist_pool.tile([P, STEP_TILES * TILE_COLS], F32, name="quad")
+            quads[k] = quad[:, 0 : steps[k][2] * TILE_COLS]
+            nc.scalar.activation(out=quads[k], in_=dist_cols(k), func=ACT.Square, bias=-1.0, scale=2.0)
 
         def multiply_cube(k):
-            cube = work.tile([P, PAIR_COLS], F32, name="cube")
+            cube = work.tile([P, STEP_TILES * TILE_COLS], F32, name="cube")
+            cubes[k] = cube[:, 0 : steps[k][2] * TILE_COLS]
             nc.vector.scalar_tensor_tensor(
-                out=cube[:], in0=dist_cols(k), scalar=0.5, in1=quads[k][:],
+                out=cubes[k], in0=dist_cols(k), scalar=0.5, in1=quads[k],
                 op0=ALU.subtract, op1=ALU.mult,
             )
-            cubes[k] = cube
 
         def clip_outer(k):
-            outer_row = work.tile([P, PAIR * 2, P, 2], BF16, name="outer_row")
-            nc.vector.tensor_scalar(
-                out=outer_row[:],
-                in0=cubes[k][:].rearrange("p (au e m) -> p au m e", e=2, m=P),
+            outer_row = work.tile([P, STEP_TILES * 2, P, 2], BF16, name="outer_row")
+            nc.gpsimd.tensor_scalar(
+                out=outer_row[:, 0 : steps[k][2] * 2],
+                in0=cubes[k].rearrange("p (au e m) -> p au m e", e=2, m=P),
                 scalar1=-1.0 / 3.0, scalar2=0.0, op0=ALU.mult, op1=ALU.max,
             )
             outer_rows[k] = outer_row
@@ -176,19 +175,23 @@ def tile_fastkanlayer_pa_t_kernel(tc, x, spline_weight, grid, out):
                 busy[:], ident_f32[:], dist_cols(0)[:, 0 : PACK * P], start=True, stop=True
             )
 
-        def transposes(k):
+        def transposes(k, pair):
             words = outer_rows[k][:].rearrange("p au m e -> p (au m e)").bitcast(F32)
-            outer_t = psum_two.tile([P, PAIR, 2, P], F32, name="outer_t")
-            for a in range(PAIR):
-                for w in range(2):
-                    at = (a * 2 + w) * P
-                    nc.tensor.transpose(outer_t[:, a, w, :], words[:, at : at + P], ident_f32[:])
-            outers[k] = outer_t
-            parts = (dist_cols(k), quads[k][:], cubes[k][:])
-            inners[k] = []
-            for a in range(PAIR):
+            parts = (dist_cols(k), quads[k], cubes[k])
+            if pair == 0:
+                inners[k] = []
+                outers[k] = []
+            for a in range(pair * PAIR, (pair + 1) * PAIR):
+                if a % PAIR == 0:
+                    outer_t = psum_two.tile([P, PAIR, 2, P], F32, name="outer_t")
+                    for n in range(PAIR * 2):
+                        at = (a * 2 + n) * P
+                        nc.tensor.transpose(
+                            outer_t[:, n // 2, n % 2, :], words[:, at : at + P], ident_f32[:]
+                        )
+                    outers[k].append(outer_t)
                 inner_t = psum_in.tile([P, PACK, P], F32, tag="inner")
-                for n in range(0 if a == 0 else UNFED_FILLS if k < UNFED_STEPS else 1):
+                for n in range(0 if a % PAIR == 0 else UNFED_FILLS if k < UNFED_STEPS else pair):
                     nc.tensor.matmul(inner_t[:, n, :], ident_f32[:], ident_f32[:], start=True, stop=True)
                 for t in range(PACK):
                     at = (a * PACK + t) * P
@@ -199,69 +202,73 @@ def tile_fastkanlayer_pa_t_kernel(tc, x, spline_weight, grid, out):
                         )
                 inners[k].append(inner_t)
 
-        def copy_outer(k):
+        def copy_outer(k, pair):
             outer_k = work.tile([P, PAIR, P, PACK], BF16, name="outer_k")
             nc.scalar.copy(
                 out=outer_k[:].rearrange("q a p t -> q (a p t)").bitcast(F32).rearrange(
                     "q (a p w) -> q a p w", a=PAIR, w=2
                 ),
-                in_=outers[k][:].rearrange("q a w p -> q a p w"),
+                in_=outers[k][pair][:].rearrange("q a w p -> q a p w"),
             )
-            outers[k] = outer_k
+            outers[k][pair] = outer_k
 
-        def minimum(k):
-            basis = work.tile([P, PAIR, P, PACK], BF16, align_bytes=64, name="basis")
+        def minimum(k, pair):
+            if pair == 0:
+                basis = work.tile([P, STEP_TILES, P, PACK], BF16, align_bytes=64, name="basis")
+                bases[k] = basis
             for a in range(PAIR):
                 nc.vector.scalar_tensor_tensor(
-                    out=basis[:, a], in0=inners[k][a][:].rearrange("q t p -> q p t"),
-                    scalar=-5.0 / 12.0, in1=outers[k][:, a], op0=ALU.add, op1=ALU.min,
+                    out=bases[k][:, pair * PAIR + a],
+                    in0=inners[k][pair * PAIR + a][:].rearrange("q t p -> q p t"),
+                    scalar=-5.0 / 12.0, in1=outers[k][pair][:, a], op0=ALU.add, op1=ALU.min,
                 )
-            bases[k] = basis
 
         def quantise(k):
-            u, j = steps[k]
-            first, tiles, h = units[u]
-            if h == 0 and j == 0:
+            u, at, tiles = steps[k]
+            first, unit_tiles, h = units[u]
+            if h == 0 and at == 0:
                 code = work.tile([P, PASSES, MAX_TILES, P], U32, align_bytes=64, name="code")
                 scale = work.tile([P, PASSES, MAX_TILES, P], U8, align_bytes=64, name="scale")
                 codes[first] = code
                 scales[first] = scale
             nc.vector.quantize_mx(
-                out=codes[first][:, h, j * PAIR : (j + 1) * PAIR].rearrange("q a p -> q (a p)").bitcast(FP8X4),
-                scales=scales[first][:, h, j * PAIR : (j + 1) * PAIR].rearrange("q a p -> q (a p)"),
-                in_=bases[k][:].rearrange("q a p t -> q (a p t)"),
+                out=codes[first][:, h, at : at + tiles].rearrange("q a p -> q (a p)").bitcast(FP8X4),
+                scales=scales[first][:, h, at : at + tiles].rearrange("q a p -> q (a p)"),
+                in_=bases[k][:, 0:tiles].rearrange("q a p t -> q (a p t)"),
             )
+            if h == PASSES - 1:
+                for n in range(at, at + tiles, PAIR):
+                    ready.append((first, n))
 
         ready = []
         done = []
 
         def multiply():
-            first, j = ready.pop(0)
+            first, n = ready.pop(0)
             acc = psum_two.tile([P, PAIR, J], F32, name="acc")
             for a in range(PAIR):
                 for h in range(PASSES):
                     nc.tensor.matmul_mx(
                         out=acc[:, a, :],
-                        lhsT=codes[first][:, h, j * PAIR + a, :].bitcast(FP8X4),
-                        lhsT_scale=scales[first][:, h, j * PAIR + a, :],
+                        lhsT=codes[first][:, h, n + a, :].bitcast(FP8X4),
+                        lhsT_scale=scales[first][:, h, n + a, :],
                         rhs=w_codes[:, h, :].bitcast(FP8X4),
                         rhs_scale=w_scales[:, h, :],
                         start=(h == 0),
                         stop=(h == PASSES - 1),
                     )
-            done.append((acc, first + j * PAIR))
+            done.append((acc, first + n))
 
-        def store():
-            acc, row = done.pop(0)
+        def store(bank):
+            acc, row = bank
             result = work.tile([P, PAIR * J], F32, name="result")
-            nc.scalar.activation(
-                out=result[:], in_=acc[:].rearrange("p a j -> p (a j)"), func=ACT.Copy, scale=8.0
+            nc.vector.tensor_scalar_mul(
+                out=result[:], in0=acc[:].rearrange("p a j -> p (a j)"), scalar1=8.0
             )
             nc.sync.dma_start(out=out_rows[:, row * J : (row + PAIR) * J], in_=result[:])
 
         for c in range(KNOTS):
             distance(0, c)
-        sort_weight()
         wake()
 
         pending = []
@@ -269,39 +276,49 @@ def tile_fastkanlayer_pa_t_kernel(tc, x, spline_weight, grid, out):
             for c in range(KNOTS):
                 pending.append((u, c))
         for k in range(-3, n_steps + 2):
-            if 0 <= k + 1 < n_steps:
-                transposes(k + 1)
+            pairs = steps[k][2] // PAIR if 0 <= k < n_steps else 0
+            turns = steps[k + 1][2] // PAIR if 0 <= k + 1 < n_steps else 0
+            due = 0
+            if 0 <= k + 3 < n_steps:
+                u, at, tiles = steps[k + 3]
+                due = KNOTS * tiles // units[u][1]
+            finished = list(done)
+            done.clear()
+            if turns > 0:
+                transposes(k + 1, 0)
+            if turns > 1:
+                transposes(k + 1, 1)
+            if ready and k >= 2 + PASSES and (turns != 1 or k % 2 == 0 or k >= n_steps - 6):
+                multiply()
+            if pairs > 0:
+                copy_outer(k, 0)
+            if pairs > 1:
+                copy_outer(k, 1)
             if 0 <= k + 3 < n_steps:
                 square(k + 3)
-            if 0 <= k + 2 < n_steps:
-                multiply_cube(k + 2)
+            if 1 <= k < 1 + PASSES:
+                turn_weight(k - 1)
             if 0 <= k - 1 < n_steps:
                 quantise(k - 1)
-                u, j = steps[k - 1]
-                if units[u][2] == PASSES - 1:
-                    ready.append((units[u][0], j))
-            if 0 <= k < n_steps:
-                copy_outer(k)
-            if 0 <= k < PASSES:
-                turn_weight(k)
-            if 0 <= k - 1 < PASSES:
-                quantise_weight(k - 1)
+            if 2 <= k < 2 + PASSES:
+                quantise_weight(k - 2)
+            if 0 <= k + 2 < n_steps:
+                multiply_cube(k + 2)
             if 0 <= k + 2 < n_steps:
                 clip_outer(k + 2)
-            if 0 <= k + 3 < n_steps:
-                u, j = steps[k + 3]
-                unit_steps = units[u][1] // PAIR
-                for n in range(KNOTS // unit_steps):
-                    if pending:
-                        unit_c, c = pending.pop(0)
-                        distance(unit_c, c)
-            while done:
-                store()
-            if 0 <= k < n_steps:
-                minimum(k)
-            if ready and (k % 2 == 0 or k >= n_steps - 4):
-                multiply()
+            if 0 <= k < 0 + PASSES:
+                sort_weight(k - 0)
+            if pairs > 0:
+                minimum(k, 0)
+            if pairs > 1:
+                minimum(k, 1)
+            for bank in finished:
+                store(bank)
+            for n in range(due):
+                if pending:
+                    unit_c, c = pending.pop(0)
+                    distance(unit_c, c)
         while ready:
             multiply()
-        while done:
-            store()
+        for bank in done:
+            store(bank)

@@ -89,7 +89,7 @@ def tile_fastkanlayer_pa_t_kernel(tc, x, spline_weight, grid, out):
 
         def turn_weight(h):
             for jh in range(J // P):
-                w_t = psum_in.tile([P, PACK, P], BF16, tag="inner")
+                w_t = psum_two.tile([P, PACK, P], BF16, tag="acc")
                 for t in range(PACK):
                     nc.tensor.transpose(w_t[:, t, :], w_sorted[:, h, jh, t, :], ident_bf16[:])
                 nc.scalar.copy(
@@ -162,7 +162,7 @@ def tile_fastkanlayer_pa_t_kernel(tc, x, spline_weight, grid, out):
 
         def clip_outer(k):
             outer_row = work.tile([P, STEP_TILES * 2, P, 2], BF16, name="outer_row")
-            nc.gpsimd.tensor_scalar(
+            nc.vector.tensor_scalar(
                 out=outer_row[:, 0 : steps[k][2] * 2],
                 in0=cubes[k].rearrange("p (au e m) -> p au m e", e=2, m=P),
                 scalar1=-1.0 / 3.0, scalar2=0.0, op0=ALU.mult, op1=ALU.max,
@@ -245,7 +245,7 @@ def tile_fastkanlayer_pa_t_kernel(tc, x, spline_weight, grid, out):
 
         def multiply():
             first, n = ready.pop(0)
-            acc = psum_two.tile([P, PAIR, J], F32, name="acc")
+            acc = psum_two.tile([P, PAIR, J], F32, tag="acc")
             for a in range(PAIR):
                 for h in range(PASSES):
                     nc.tensor.matmul_mx(
@@ -262,8 +262,8 @@ def tile_fastkanlayer_pa_t_kernel(tc, x, spline_weight, grid, out):
         def store(bank):
             acc, row = bank
             result = work.tile([P, PAIR * J], F32, name="result")
-            nc.vector.tensor_scalar_mul(
-                out=result[:], in0=acc[:].rearrange("p a j -> p (a j)"), scalar1=8.0
+            nc.scalar.activation(
+                out=result[:], in_=acc[:].rearrange("p a j -> p (a j)"), func=ACT.Copy, scale=8.0
             )
             nc.sync.dma_start(out=out_rows[:, row * J : (row + PAIR) * J], in_=result[:])
 
@@ -288,8 +288,10 @@ def tile_fastkanlayer_pa_t_kernel(tc, x, spline_weight, grid, out):
                 transposes(k + 1, 0)
             if turns > 1:
                 transposes(k + 1, 1)
-            if ready and k >= 2 + PASSES and (turns != 1 or k % 2 == 0 or k >= n_steps - 6):
-                multiply()
+            if k >= 3 + PASSES:
+                for n in range(2 if k >= n_steps - 6 else 1 if turns != 1 or k % 2 == 0 else 0):
+                    if ready:
+                        multiply()
             if pairs > 0:
                 copy_outer(k, 0)
             if pairs > 1:
@@ -300,24 +302,24 @@ def tile_fastkanlayer_pa_t_kernel(tc, x, spline_weight, grid, out):
                 turn_weight(k - 1)
             if 0 <= k - 1 < n_steps:
                 quantise(k - 1)
-            if 2 <= k < 2 + PASSES:
-                quantise_weight(k - 2)
+            if 3 <= k < 3 + PASSES:
+                quantise_weight(k - 3)
             if 0 <= k + 2 < n_steps:
                 multiply_cube(k + 2)
-            if 0 <= k + 2 < n_steps:
-                clip_outer(k + 2)
-            if 0 <= k < 0 + PASSES:
-                sort_weight(k - 0)
             if pairs > 0:
                 minimum(k, 0)
+            if 0 <= k < 0 + PASSES:
+                sort_weight(k - 0)
             if pairs > 1:
                 minimum(k, 1)
-            for bank in finished:
-                store(bank)
+            if 0 <= k + 2 < n_steps:
+                clip_outer(k + 2)
             for n in range(due):
                 if pending:
                     unit_c, c = pending.pop(0)
                     distance(unit_c, c)
+            for bank in finished:
+                store(bank)
         while ready:
             multiply()
         for bank in done:

@@ -31,7 +31,7 @@ UNFED_FILLS = 3
 
 CHUNKS = (2, 2, 4, 8, 8, 8, 8, 8, 8, 4, 4)
 MAX_TILES = max(CHUNKS)
-STEP_TILES = 4
+STEP_TILES = 2
 
 
 def tile_fastkanlayer_pa_t_kernel(tc, x, spline_weight, grid, out):
@@ -113,7 +113,7 @@ def tile_fastkanlayer_pa_t_kernel(tc, x, spline_weight, grid, out):
         steps = []
         for u in range(len(units)):
             tiles_of_u = units[u][1]
-            step = STEP_TILES if tiles_of_u == MAX_TILES else PAIR
+            step = STEP_TILES
             for at in range(0, tiles_of_u, step):
                 steps.append((u, at, step))
         n_steps = len(steps)
@@ -191,7 +191,7 @@ def tile_fastkanlayer_pa_t_kernel(tc, x, spline_weight, grid, out):
                         )
                     outers[k].append(outer_t)
                 inner_t = psum_in.tile([P, PACK, P], F32, tag="inner")
-                for n in range(0 if a % PAIR == 0 else UNFED_FILLS if k < UNFED_STEPS else pair):
+                for n in range(0 if a % PAIR == 0 else UNFED_FILLS if k < UNFED_STEPS else 1):
                     nc.tensor.matmul(inner_t[:, n, :], ident_f32[:], ident_f32[:], start=True, stop=True)
                 for t in range(PACK):
                     at = (a * PACK + t) * P
@@ -286,16 +286,12 @@ def tile_fastkanlayer_pa_t_kernel(tc, x, spline_weight, grid, out):
             done.clear()
             if turns > 0:
                 transposes(k + 1, 0)
-            if turns > 1:
-                transposes(k + 1, 1)
             if k >= 3 + PASSES:
-                for n in range(2 if k >= n_steps - 6 else 1 if turns != 1 or k % 2 == 0 else 0):
+                for n in range(1 if k % 2 == 0 or k >= n_steps - 6 else 0):
                     if ready:
                         multiply()
             if pairs > 0:
                 copy_outer(k, 0)
-            if pairs > 1:
-                copy_outer(k, 1)
             if 0 <= k + 3 < n_steps:
                 square(k + 3)
             if 1 <= k < 1 + PASSES:
@@ -306,12 +302,10 @@ def tile_fastkanlayer_pa_t_kernel(tc, x, spline_weight, grid, out):
                 quantise_weight(k - 3)
             if 0 <= k + 2 < n_steps:
                 multiply_cube(k + 2)
-            if pairs > 0:
-                minimum(k, 0)
             if 0 <= k < 0 + PASSES:
                 sort_weight(k - 0)
-            if pairs > 1:
-                minimum(k, 1)
+            if pairs > 0:
+                minimum(k, 0)
             if 0 <= k + 2 < n_steps:
                 clip_outer(k + 2)
             for n in range(due):

@@ -29,7 +29,7 @@ TILE_COLS = P * PACK
 UNFED_STEPS = 5
 UNFED_FILLS = 3
 
-CHUNKS = (2, 2, 4, 8, 8, 8, 8, 8, 8, 4, 4)
+CHUNKS = (4, 8, 8, 8, 8, 8, 8, 8, 4)
 MAX_TILES = max(CHUNKS)
 STEP_TILES = 2
 
@@ -241,6 +241,7 @@ def tile_fastkanlayer_pa_t_kernel(tc, x, spline_weight, grid, out):
                     ready.append((first, n))
 
         ready = []
+        aged = []
         done = []
 
         def multiply():
@@ -281,8 +282,10 @@ def tile_fastkanlayer_pa_t_kernel(tc, x, spline_weight, grid, out):
             due = 0
             if 0 <= k + 3 < n_steps:
                 u, at, tiles = steps[k + 3]
-                due = KNOTS * tiles // units[u][1]
-            finished = list(done)
+                due = KNOTS * (at + tiles) // units[u][1] - KNOTS * at // units[u][1]
+            finished = list(aged)
+            aged.clear()
+            aged.extend(done)
             done.clear()
             if turns > 0:
                 transposes(k + 1, 0)
@@ -290,10 +293,10 @@ def tile_fastkanlayer_pa_t_kernel(tc, x, spline_weight, grid, out):
                 for n in range(1 if k % 2 == 0 or k >= n_steps - 6 else 0):
                     if ready:
                         multiply()
-            if pairs > 0:
-                copy_outer(k, 0)
             if 0 <= k + 3 < n_steps:
                 square(k + 3)
+            if turns > 0:
+                copy_outer(k + 1, 0)
             if 1 <= k < 1 + PASSES:
                 turn_weight(k - 1)
             if 0 <= k - 1 < n_steps:
@@ -316,5 +319,5 @@ def tile_fastkanlayer_pa_t_kernel(tc, x, spline_weight, grid, out):
                 store(bank)
         while ready:
             multiply()
-        for bank in done:
+        for bank in aged + done:
             store(bank)

from contextlib import ExitStack

import concourse.mybir as mybir
from concourse.masks import make_identity

F32 = mybir.dt.float32
BF16 = mybir.dt.bfloat16
U32 = mybir.dt.uint32
U8 = mybir.dt.uint8
FP8X4 = mybir.dt.float8_e4m3fn_x4
ALU = mybir.AluOpType
ACT = mybir.ActivationFunctionType

B, I, J, C = 8192, 32, 256, 32
K = C * I
FLOPS = 2 * B * K * J

P = 128
PACK = 4
K_PASS = P * PACK
PASSES = K // K_PASS
KNOTS = K_PASS // I
ROWS = I // PACK
INV_H = (C - 1) / 2.0
CLIP = 0.99
N_PER_P = B // P
PAIR = 2
TILE_COLS = P * PACK
UNFED_STEPS = 5
UNFED_FILLS = 3

CHUNKS = (4, 8, 8, 8, 8, 8, 8, 8, 4)
MAX_TILES = max(CHUNKS)
STEP_TILES = 2


def tile_fastkanlayer_pa_t_kernel(tc, x, spline_weight, grid, out):
    nc = tc.nc
    out_rows = out.rearrange("(p n) j -> p (n j)", n=N_PER_P)
    x_view = x.rearrange("(p n) i -> p (n i)", n=N_PER_P)

    with ExitStack() as ctx:
        keep = ctx.enter_context(tc.tile_pool(name="keep", bufs=1))
        dist_pool = ctx.enter_context(tc.tile_pool(name="dist_pool", bufs=4))
        work = ctx.enter_context(tc.tile_pool(name="work", bufs=3))
        psum_in = ctx.enter_context(tc.psum_pool(name="psum_in", bufs=4))
        psum_two = ctx.enter_context(tc.psum_pool(name="psum_two", bufs=2))
        ctx.enter_context(tc.manual_schedule())

        warm = keep.tile([P, 1], F32)
        nc.vector.memset(warm[:], 0.0)
        grid_rows = keep.tile([P, C], BF16)
        nc.sync.dma_start(out=grid_rows[:], in_=grid.partition_broadcast(P))
        x_rows = keep.tile([P, N_PER_P * I], BF16)
        x_splits = (0, 4 * I, 16 * I, N_PER_P * I)
        for lo, hi in zip(x_splits[:-1], x_splits[1:]):
            nc.sync.dma_start(out=x_rows[:, lo:hi], in_=x_view[:, lo:hi])
        w_rows = keep.tile([P, I, J // P, C], BF16)
        nc.sync.dma_start(
            out=w_rows[:], in_=spline_weight.rearrange("i (jh jl) c -> jl i jh c", jl=P)
        )
        nc.scalar.activation(out=warm[:], in_=warm[:], func=ACT.Abs)
        ident_f32 = keep.tile([P, P], F32)
        make_identity(nc, ident_f32[:])
        ident_bf16 = keep.tile([P, P], BF16)
        make_identity(nc, ident_bf16[:])

        neg_knot = keep.tile([P, C], F32)
        nc.vector.tensor_scalar_mul(out=neg_knot[:], in0=grid_rows[:], scalar1=-INV_H / 4.0)
        x_clip = keep.tile([P, N_PER_P * I], F32)
        for lo, hi in zip(x_splits[:-1], x_splits[1:]):
            nc.vector.tensor_scalar(
                out=x_clip[:, lo:hi], in0=x_rows[:, lo:hi],
                scalar1=CLIP, scalar2=-CLIP, op0=ALU.min, op1=ALU.max,
            )

        w_codes = keep.tile([P, PASSES, J], U32, align_bytes=64)
        w_scales = keep.tile([P, PASSES, J], U8, align_bytes=64)
        w_by_pass = w_rows[:].rearrange("p (t r) jh (h c) -> p h jh t c r", t=PACK, h=PASSES)
        w_sorted = keep.tile([P, PASSES, J // P, PACK, P], BF16)
        w_grouped = keep.tile([P, PASSES, J, PACK], BF16, align_bytes=64)

        def sort_weight(h):
            for jh in range(J // P):
                nc.vector.tensor_copy(
                    out=w_sorted[:, h, jh].rearrange("p t (c r) -> p t c r", r=ROWS),
                    in_=w_by_pass[:, h, jh],
                )

        def turn_weight(h):
            for jh in range(J // P):
                w_t = psum_two.tile([P, PACK, P], BF16, tag="acc")
                for t in range(PACK):
                    nc.tensor.transpose(w_t[:, t, :], w_sorted[:, h, jh, t, :], ident_bf16[:])
                nc.scalar.copy(
                    out=w_grouped[:, h, jh * P : (jh + 1) * P, :],
                    in_=w_t[:].rearrange("q t j -> q j t"),
                )

        def quantise_weight(h):
            nc.vector.quantize_mx(
                out=w_codes[:, h, :].bitcast(FP8X4),
                scales=w_scales[:, h, :],
                in_=w_grouped[:, h].rearrange("q j t -> q (j t)"),
            )

        units = []
        first_tile = 0
        for tiles in CHUNKS:
            for h in range(PASSES):
                units.append((first_tile, tiles, h))
            first_tile += tiles
        steps = []
        for u in range(len(units)):
            tiles_of_u = units[u][1]
            step = STEP_TILES
            for at in range(0, tiles_of_u, step):
                steps.append((u, at, step))
        n_steps = len(steps)

        dists = {}
        quads = {}
        cubes = {}
        outer_rows = {}
        inners = {}
        outers = {}
        bases = {}
        codes = {}
        scales = {}

        def distance(u, c):
            first, tiles, h = units[u]
            if u not in dists:
                dist_u = dist_pool.tile([P, MAX_TILES, PACK, KNOTS, ROWS], F32, name="dist_u")
                dists[u] = dist_u
            nc.scalar.activation(
                out=dists[u][:, 0:tiles, :, c, :],
                in_=x_clip[:, first * I : (first + tiles) * I].rearrange(
                    "p (a t r) -> p a t r", t=PACK, r=ROWS
                ),
                func=ACT.Abs,
                bias=neg_knot[:, h * KNOTS + c : h * KNOTS + c + 1],
                scale=INV_H / 4.0,
            )

        def dist_cols(k):
            u, at, tiles = steps[k]
            return dists[u][:, at : at + tiles].rearrange("p a t c r -> p (a t c r)")

        def square(k):
            quad = dist_pool.tile([P, STEP_TILES * TILE_COLS], F32, name="quad")
            quads[k] = quad[:, 0 : steps[k][2] * TILE_COLS]
            nc.scalar.activation(out=quads[k], in_=dist_cols(k), func=ACT.Square, bias=-1.0, scale=2.0)

        def multiply_cube(k):
            cube = work.tile([P, STEP_TILES * TILE_COLS], F32, name="cube")
            cubes[k] = cube[:, 0 : steps[k][2] * TILE_COLS]
            nc.vector.scalar_tensor_tensor(
                out=cubes[k], in0=dist_cols(k), scalar=0.5, in1=quads[k],
                op0=ALU.subtract, op1=ALU.mult,
            )

        def clip_outer(k):
            outer_row = work.tile([P, STEP_TILES * 2, P, 2], BF16, name="outer_row")
            nc.vector.tensor_scalar(
                out=outer_row[:, 0 : steps[k][2] * 2],
                in0=cubes[k].rearrange("p (au e m) -> p au m e", e=2, m=P),
                scalar1=-1.0 / 3.0, scalar2=0.0, op0=ALU.mult, op1=ALU.max,
            )
            outer_rows[k] = outer_row

        def wake():
            busy = psum_in.tile([P, PACK * P], F32, tag="inner")
            nc.tensor.matmul(
                busy[:], ident_f32[:], dist_cols(0)[:, 0 : PACK * P], start=True, stop=True
            )

        def transposes(k, pair):
            words = outer_rows[k][:].rearrange("p au m e -> p (au m e)").bitcast(F32)
            parts = (dist_cols(k), quads[k], cubes[k])
            if pair == 0:
                inners[k] = []
                outers[k] = []
            for a in range(pair * PAIR, (pair + 1) * PAIR):
                if a % PAIR == 0:
                    outer_t = psum_two.tile([P, PAIR, 2, P], F32, name="outer_t")
                    for n in range(PAIR * 2):
                        at = (a * 2 + n) * P
                        nc.tensor.transpose(
                            outer_t[:, n // 2, n % 2, :], words[:, at : at + P], ident_f32[:]
                        )
                    outers[k].append(outer_t)
                inner_t = psum_in.tile([P, PACK, P], F32, tag="inner")
                for n in range(0 if a % PAIR == 0 else UNFED_FILLS if k < UNFED_STEPS else 1):
                    nc.tensor.matmul(inner_t[:, n, :], ident_f32[:], ident_f32[:], start=True, stop=True)
                for t in range(PACK):
                    at = (a * PACK + t) * P
                    for n, part in enumerate(parts):
                        nc.tensor.matmul(
                            inner_t[:, t, :], part[:, at : at + P], ident_f32[:],
                            start=(n == 0), stop=(n == len(parts) - 1), is_transpose=True,
                        )
                inners[k].append(inner_t)

        def copy_outer(k, pair):
            outer_k = work.tile([P, PAIR, P, PACK], BF16, name="outer_k")
            nc.scalar.copy(
                out=outer_k[:].rearrange("q a p t -> q (a p t)").bitcast(F32).rearrange(
                    "q (a p w) -> q a p w", a=PAIR, w=2
                ),
                in_=outers[k][pair][:].rearrange("q a w p -> q a p w"),
            )
            outers[k][pair] = outer_k

        def minimum(k, pair):
            if pair == 0:
                basis = work.tile([P, STEP_TILES, P, PACK], BF16, align_bytes=64, name="basis")
                bases[k] = basis
            for a in range(PAIR):
                nc.vector.scalar_tensor_tensor(
                    out=bases[k][:, pair * PAIR + a],
                    in0=inners[k][pair * PAIR + a][:].rearrange("q t p -> q p t"),
                    scalar=-5.0 / 12.0, in1=outers[k][pair][:, a], op0=ALU.add, op1=ALU.min,
                )

        def quantise(k):
            u, at, tiles = steps[k]
            first, unit_tiles, h = units[u]
            if h == 0 and at == 0:
                code = work.tile([P, PASSES, MAX_TILES, P], U32, align_bytes=64, name="code")
                scale = work.tile([P, PASSES, MAX_TILES, P], U8, align_bytes=64, name="scale")
                codes[first] = code
                scales[first] = scale
            nc.vector.quantize_mx(
                out=codes[first][:, h, at : at + tiles].rearrange("q a p -> q (a p)").bitcast(FP8X4),
                scales=scales[first][:, h, at : at + tiles].rearrange("q a p -> q (a p)"),
                in_=bases[k][:, 0:tiles].rearrange("q a p t -> q (a p t)"),
            )
            if h == PASSES - 1:
                for n in range(at, at + tiles, PAIR):
                    ready.append((first, n))

        ready = []
        aged = []
        done = []

        def multiply():
            first, n = ready.pop(0)
            acc = psum_two.tile([P, PAIR, J], F32, tag="acc")
            for a in range(PAIR):
                for h in range(PASSES):
                    nc.tensor.matmul_mx(
                        out=acc[:, a, :],
                        lhsT=codes[first][:, h, n + a, :].bitcast(FP8X4),
                        lhsT_scale=scales[first][:, h, n + a, :],
                        rhs=w_codes[:, h, :].bitcast(FP8X4),
                        rhs_scale=w_scales[:, h, :],
                        start=(h == 0),
                        stop=(h == PASSES - 1),
                    )
            done.append((acc, first + n))

        def store(bank):
            acc, row = bank
            result = work.tile([P, PAIR * J], F32, name="result")
            nc.scalar.activation(
                out=result[:], in_=acc[:].rearrange("p a j -> p (a j)"), func=ACT.Copy, scale=8.0
            )
            nc.sync.dma_start(out=out_rows[:, row * J : (row + PAIR) * J], in_=result[:])

        for c in range(KNOTS):
            distance(0, c)
        wake()

        pending = []
        for u in range(1, len(units)):
            for c in range(KNOTS):
                pending.append((u, c))
        for k in range(-3, n_steps + 2):
            pairs = steps[k][2] // PAIR if 0 <= k < n_steps else 0
            turns = steps[k + 1][2] // PAIR if 0 <= k + 1 < n_steps else 0
            due = 0
            if 0 <= k + 3 < n_steps:
                u, at, tiles = steps[k + 3]
                due = KNOTS * (at + tiles) // units[u][1] - KNOTS * at // units[u][1]
            finished = list(aged)
            aged.clear()
            aged.extend(done)
            done.clear()
            if turns > 0:
                transposes(k + 1, 0)
            if k >= 3 + PASSES:
                for n in range(1 if k % 2 == 0 or k >= n_steps - 6 else 0):
                    if ready:
                        multiply()
            if 0 <= k + 3 < n_steps:
                square(k + 3)
            if turns > 0:
                copy_outer(k + 1, 0)
            if 1 <= k < 1 + PASSES:
                turn_weight(k - 1)
            if 0 <= k - 1 < n_steps:
                quantise(k - 1)
            if 3 <= k < 3 + PASSES:
                quantise_weight(k - 3)
            if 0 <= k + 2 < n_steps:
                multiply_cube(k + 2)
            if 0 <= k < 0 + PASSES:
                sort_weight(k - 0)
            if pairs > 0:
                minimum(k, 0)
            if 0 <= k + 2 < n_steps:
                clip_outer(k + 2)
            for n in range(due):
                if pending:
                    unit_c, c = pending.pop(0)
                    distance(unit_c, c)
            for bank in finished:
                store(bank)
        while ready:
            multiply()
        for bank in aged + done:
            store(bank)
